import numpy as np
import ml_dtypes


def mxq(x, axis, fmt="e4m3"):
    dtype, down = {"e4m3": (ml_dtypes.float8_e4m3fn, 7), "e5m2": (ml_dtypes.float8_e5m2, 14)}[fmt]
    v = np.moveaxis(np.asarray(x, np.float32).astype(ml_dtypes.bfloat16).astype(np.float64), axis, -1)
    blocks = v.reshape(v.shape[:-1] + (-1, 32))
    amax = np.abs(blocks).max(-1, keepdims=True)
    byte = np.maximum(np.where(amax > 0, np.frexp(amax)[1] - 1 + 127, 0) - down, 1)
    scale = np.exp2(byte - 127.0)
    codes = (blocks / scale).astype(np.float32).astype(dtype).astype(np.float64)
    return np.moveaxis((codes * scale).reshape(v.shape), -1, axis)


WIDE = False


def mx_kscale(k):
    if not WIDE:
        return np.ones(k)
    levels = np.array([10, -10, 5, -5, 0])
    a = np.random.permutation(np.resize(levels, k // 512 * 4)).reshape(k // 512, 4)
    idx = np.arange(k)
    return np.exp2(a[idx // 512, idx % 128 // 32])


BF16 = ml_dtypes.bfloat16


def bf(x):
    return np.asarray(x, np.float32).astype(BF16)


def f64(x):
    return np.asarray(x).astype(np.float64)


B, D, L = 8192, 512, 4


def relu(v):
    return np.maximum(v, 0.0)


def setup_inputs():
    s = mx_kscale(D)
    return {"h_prev": bf(relu(np.random.standard_normal((B, D))) * s),
            "x": bf(np.random.standard_normal((B, D)) * 1.5 / np.sqrt(np.sqrt(D))),
            "w_last": bf(np.random.standard_normal((D, D)) * 2.0 / np.sqrt(D) / s[None, :]),
            "b_last": bf(np.random.standard_normal(D) * 0.2),
            "w_out": bf(np.random.standard_normal((D, D)) / np.sqrt(D)),
            "b_out": bf(np.random.standard_normal(D) * 0.2)}


def reference(h_prev, x, w_last, b_last, w_out, b_out):
    xf = f64(x)
    interactions = relu(xf * xf.sum(axis=1, keepdims=True))
    h = relu((mxq(f64(h_prev), 1, "e4m3") @ mxq(f64(w_last), 1, "e4m3").T) + f64(b_last))
    z = (h + interactions) * 0.5
    return (mxq(z, 1, "e4m3") @ mxq(f64(w_out), 1, "e4m3").T) + f64(b_out)

@@ -1,0 +1,328 @@
+from contextlib import ExitStack
+
+import concourse.masks as masks
+import concourse.mybir as mybir
+
+F32 = mybir.dt.float32
+BF16 = mybir.dt.bfloat16
+I32 = mybir.dt.int32
+U32 = mybir.dt.uint32
+U8 = mybir.dt.uint8
+FP8X4 = mybir.dt.float8_e4m3fn_x4
+ALU = mybir.AluOpType
+ACT = mybir.ActivationFunctionType
+
+P = 128
+B = 8192
+D = 512
+FLOPS = 2 * 2 * B * D * D
+
+GROUP = 512
+NG = B // GROUP
+NH = 2 * NG
+LOOKAHEAD = 3
+
+LAG_ROW = 1
+LAG_MM1 = 2
+LAG_S1 = 3
+LAG_T = 5
+LAG_QZ = 6
+LAG_MM2 = 6
+LAG_V4 = 7
+
+
+def tile_deepfm_pa_t_kernel(tc, h_prev, x, w_last, b_last, w_out, b_out, out):
+    nc = tc.nc
+    with ExitStack() as ctx:
+        const = ctx.enter_context(tc.tile_pool(name="const", bufs=1))
+        io = ctx.enter_context(tc.tile_pool(name="io", bufs=4))
+        work = ctx.enter_context(tc.tile_pool(name="work", bufs=2))
+        psum = ctx.enter_context(tc.psum_pool(name="psum", bufs=2))
+        ctx.enter_context(tc.manual_schedule())
+
+        h_in = {}
+        x_in = {}
+
+        def load(g):
+            rows = slice(GROUP * g, GROUP * (g + 1))
+            h_t = io.tile([P, 4 * D], BF16, name="h_t", tag="h_in", bufs=4)
+            nc.sync.dma_start(out=h_t[:], in_=h_prev[rows, :].rearrange("(p j) k -> p (j k)", j=4))
+            x_t = io.tile([P, 4 * D], BF16, name="x_t", tag="x_in", bufs=5)
+            nc.sync.dma_start(out=x_t[:], in_=x[rows, :].rearrange("(p j) k -> p (j k)", j=4))
+            h_in[g] = h_t
+            x_in[g] = x_t
+
+        w1_raw = const.tile([P, 4 * D], BF16, name="w1_raw")
+        nc.sync.dma_start(
+            out=w1_raw[:].rearrange("p (ob k) -> p ob k", ob=4),
+            in_=w_last.rearrange("(ob p) k -> p ob k", p=P),
+        )
+        load(0)
+        bl_bf = const.tile([P, P], BF16, name="bl_bf")
+        nc.vector.memset(bl_bf[:].bitcast(I32), 0)
+        nc.sync.dma_start(out=bl_bf[0:4, :], in_=b_last.rearrange("(t p) -> t p", p=P))
+        w2_raw = const.tile([P, 4 * D], BF16, name="w2_raw")
+        nc.sync.dma_start(
+            out=w2_raw[:].rearrange("p (ob k) -> p ob k", ob=4),
+            in_=w_out.rearrange("(ob p) k -> p ob k", p=P),
+        )
+        load(1)
+        load(2)
+
+        ident = const.tile([P, P], F32, name="ident")
+        masks.make_identity(nc, ident[:])
+        bo = const.tile([P, D], BF16, name="bo")
+        nc.sync.dma_start(out=bo[:], in_=b_out.partition_broadcast(P))
+
+        def words_to_psum(src_words, half):
+            bank = psum.tile([P, 512], F32, name="hbank", tag="H")
+            for jj in range(2):
+                for u in range(2):
+                    col = (2 * half + jj) * 256 + 128 * u
+                    dst = (2 * jj + u) * 128
+                    nc.tensor.transpose(
+                        out=bank[:, dst : dst + 128],
+                        in_=src_words[:, col : col + 128],
+                        identity=ident[:],
+                    )
+            return bank
+
+        def words_out(bank, grouped, half):
+            nc.scalar.copy(
+                out=grouped[:].bitcast(F32)[:, 512 * half : 512 * half + 512].rearrange(
+                    "p (j b u) -> p j b u", j=2, u=2
+                ),
+                in_=bank[:].rearrange("p (j u b) -> p j b u", j=2, u=2),
+            )
+
+        def f32_to_psum(src, jj):
+            bank = psum.tile([P, 512], F32, name="tbank", tag="T")
+            for t in range(4):
+                nc.tensor.transpose(
+                    out=bank[:, 128 * t : 128 * t + 128],
+                    in_=src[:, 512 * jj + 128 * t : 512 * jj + 128 * t + 128],
+                    identity=ident[:],
+                )
+            return bank
+
+        gw1 = const.tile([P, 4 * D], BF16, name="gw1", align_bytes=64)
+        w1w = const.tile([P, D], U32, name="w1w", align_bytes=64)
+        w1s = const.tile([P, D], U8, name="w1s", align_bytes=64)
+        for half in range(2):
+            wb = words_to_psum(w1_raw[:].bitcast(F32), half)
+            words_out(wb, gw1, half)
+        nc.vector.quantize_mx(out=w1w[:].bitcast(FP8X4), scales=w1s[:], in_=gw1[:])
+
+        bl_f = const.tile([P, P], F32, name="bl_f")
+        nc.vector.tensor_copy(out=bl_f[:], in_=bl_bf[:])
+        bh = const.tile([P, 4], F32, name="bh")
+
+        gw2 = const.tile([P, 4 * D], BF16, name="gw2", align_bytes=64)
+        w2w = const.tile([P, D], U32, name="w2w", align_bytes=64)
+        w2s = const.tile([P, D], U8, name="w2s", align_bytes=64)
+        w2f = {}
+        for half in range(2):
+            wf = work.tile([P, 2 * D], F32, name="wf", tag="t", bufs=6)
+            nc.gpsimd.tensor_scalar(
+                out=wf[:], in0=w2_raw[:, 1024 * half : 1024 * half + 1024],
+                scalar1=1.0, scalar2=0.0, op0=ALU.mult, op1=ALU.add,
+            )
+            w2f[half] = wf
+
+        hbank = {}
+        gh = {}
+        hw = {}
+        hs = {}
+        abank = {}
+        hp = {}
+        ssum = {}
+        tnat = {}
+        tbank = {}
+        zg = {}
+        zw = {}
+        zs = {}
+        obank = {}
+        osb = {}
+
+        def pe_hT(d):
+            hbank[d] = words_to_psum(h_in[d // 2][:].bitcast(F32), d % 2)
+
+        def s_hT_out(d):
+            g = d // 2
+            if d % 2 == 0:
+                gh_t = work.tile([P, 4 * D], BF16, name="gh_t", tag="gh", bufs=2, align_bytes=64)
+                gh[g] = gh_t
+            words_out(hbank[d], gh[g], d % 2)
+
+        def v_quant_h(g):
+            hw_t = work.tile([P, D], U32, name="hw_t", tag="hw", bufs=2, align_bytes=64)
+            hs_t = work.tile([P, D], U8, name="hs_t", tag="hs", bufs=2, align_bytes=64)
+            nc.vector.quantize_mx(out=hw_t[:].bitcast(FP8X4), scales=hs_t[:], in_=gh[g][:])
+            hw[g] = hw_t
+            hs[g] = hs_t
+
+        def pe_mm1(d):
+            g = d // 2
+            for t in (2 * (d % 2), 2 * (d % 2) + 1):
+                acc = psum.tile([P, 512], F32, name="acc", tag="A")
+                nc.tensor.matmul_mx(
+                    out=acc[:],
+                    lhsT=w1w[:, 128 * t : 128 * t + 128].bitcast(FP8X4),
+                    lhsT_scale=w1s[:, 128 * t : 128 * t + 128],
+                    rhs=hw[g][:].bitcast(FP8X4),
+                    rhs_scale=hs[g][:],
+                    start=True,
+                    stop=True,
+                )
+                abank[(g, t)] = acc
+
+        def s_relu(d):
+            g = d // 2
+            if d % 2 == 0:
+                hp_t = work.tile([P, 4 * D], F32, name="hp_t", tag="hp", bufs=3)
+                hp[g] = hp_t
+            for t in (2 * (d % 2), 2 * (d % 2) + 1):
+                nc.scalar.activation(
+                    out=hp[g][:, 512 * t : 512 * t + 512],
+                    in_=abank[(g, t)][:],
+                    func=ACT.Relu,
+                    bias=bh[:, t : t + 1],
+                    scale=0.5,
+                )
+
+        def s_rowsum(d):
+            g = d // 2
+            s_t = work.tile([P, 2], F32, name="s_t", tag="s", bufs=4)
+            for jj in range(2):
+                j = 2 * (d % 2) + jj
+                junk = work.tile([P, D], BF16, name="junk", tag="junk", bufs=2)
+                nc.scalar.activation(
+                    out=junk[:],
+                    in_=x_in[g][:, 512 * j : 512 * j + 512],
+                    func=ACT.Copy,
+                    scale=0.5,
+                    accum_out=s_t[:, jj : jj + 1],
+                )
+            ssum[d] = s_t
+
+        def g_scale(d):
+            g = d // 2
+            t_t = work.tile([P, 2 * D], F32, name="t_t", tag="t", bufs=6)
+            for jj in range(2):
+                j = 2 * (d % 2) + jj
+                nc.gpsimd.tensor_scalar(
+                    out=t_t[:, 512 * jj : 512 * jj + 512],
+                    in0=x_in[g][:, 512 * j : 512 * j + 512],
+                    scalar1=ssum[d][:, jj : jj + 1],
+                    scalar2=0.0,
+                    op0=ALU.mult,
+                    op1=ALU.add,
+                )
+            tnat[d] = t_t
+
+        def pe_tT(d):
+            for jj in range(2):
+                tbank[(d, jj)] = f32_to_psum(tnat[d], jj)
+
+        def v_combine(d):
+            g = d // 2
+            zg_t = work.tile([P, 2 * D], BF16, name="zg_t", tag="zg", bufs=3, align_bytes=64)
+            for jj in range(2):
+                j = 2 * (d % 2) + jj
+                nc.vector.scalar_tensor_tensor(
+                    out=zg_t[:, 512 * jj : 512 * jj + 512].rearrange("p (b t) -> p b t", t=4),
+                    in0=tbank[(d, jj)][:].rearrange("p (t b) -> p b t", t=4),
+                    scalar=0.0,
+                    in1=hp[g][:].rearrange("p (t c) -> p t c", t=4)[:, :, 128 * j : 128 * j + 128].rearrange(
+                        "p t b -> p b t"
+                    ),
+                    op0=ALU.max,
+                    op1=ALU.add,
+                )
+            zg[d] = zg_t
+
+        def v_quant_z(d):
+            zw_t = work.tile([P, 256], U32, name="zw_t", tag="zw", bufs=3, align_bytes=64)
+            zs_t = work.tile([P, 256], U8, name="zs_t", tag="zs", bufs=3, align_bytes=64)
+            nc.vector.quantize_mx(out=zw_t[:].bitcast(FP8X4), scales=zs_t[:], in_=zg[d][:])
+            zw[d] = zw_t
+            zs[d] = zs_t
+
+        def pe_mm2(d):
+            for jj in range(2):
+                acc2 = psum.tile([P, 512], F32, name="acc2", tag="O")
+                nc.tensor.matmul_mx(
+                    out=acc2[:],
+                    lhsT=zw[d][:, 128 * jj : 128 * jj + 128].bitcast(FP8X4),
+                    lhsT_scale=zs[d][:, 128 * jj : 128 * jj + 128],
+                    rhs=w2w[:].bitcast(FP8X4),
+                    rhs_scale=w2s[:],
+                    start=True,
+                    stop=True,
+                )
+                obank[(d, jj)] = acc2
+
+        def v_bias_out(d, jj):
+            if jj == 0:
+                o_t = io.tile([P, 2 * D], F32, name="o_t", tag="o", bufs=4)
+                osb[d] = o_t
+            nc.vector.tensor_tensor(
+                out=osb[d][:, 512 * jj : 512 * jj + 512],
+                in0=obank[(d, jj)][:],
+                in1=bo[:],
+                op=ALU.add,
+            )
+
+        def store(d):
+            g = d // 2
+            r = d % 2
+            nc.sync.dma_start(
+                out=out[GROUP * g : GROUP * (g + 1), :].rearrange("(p j) o -> p j o", j=4)[:, 2 * r : 2 * r + 2, :],
+                in_=osb[d][:].rearrange("p (j o) -> p j o", j=2),
+            )
+
+        def live(d):
+            return 0 <= d < NH
+
+        for i in range(NH + LAG_V4):
+            if i % 2 == 0 and i // 2 + LOOKAHEAD < NG:
+                load(i // 2 + LOOKAHEAD)
+            if live(i - LAG_V4):
+                v_bias_out(i - LAG_V4, 0)
+            if live(i - LAG_QZ):
+                v_quant_z(i - LAG_QZ)
+            if live(i - LAG_V4):
+                v_bias_out(i - LAG_V4, 1)
+                store(i - LAG_V4)
+            if i % 2 == 0 and live(i - 2):
+                v_quant_h((i - 2) // 2)
+            if live(i - LAG_S1):
+                s_relu(i - LAG_S1)
+            if live(i - LAG_T):
+                pe_tT(i - LAG_T)
+            if i == 1:
+                tb = psum.tile([P, 512], F32, name="tb", tag="T")
+                nc.tensor.transpose(out=tb[:, 0:128], in_=bl_f[:], identity=ident[:])
+                nc.vector.tensor_scalar(out=bh[:], in0=tb[:, 0:4], scalar1=0.5, scalar2=None, op0=ALU.mult)
+            if 1 <= i <= 4:
+                ob = i - 1
+                wbank = f32_to_psum(w2f[ob // 2], ob % 2)
+                nc.vector.tensor_copy(
+                    out=gw2[:, 512 * ob : 512 * ob + 512].rearrange("p (o t) -> p o t", t=4),
+                    in_=wbank[:].rearrange("p (t o) -> p o t", t=4),
+                )
+            if i == 5:
+                nc.vector.quantize_mx(out=w2w[:].bitcast(FP8X4), scales=w2s[:], in_=gw2[:])
+            if live(i):
+                pe_hT(i)
+            if live(i - LAG_ROW):
+                s_rowsum(i - LAG_ROW)
+                g_scale(i - LAG_ROW)
+            if live(i):
+                s_hT_out(i)
+            if live(i - LAG_T):
+                v_combine(i - LAG_T)
+            if live(i - LAG_MM1):
+                pe_mm1(i - LAG_MM1)
+            if live(i - LAG_MM2):
+                pe_mm2(i - LAG_MM2)

@@ -161,9 +161,9 @@ def tile_deepfm_pa_t_kernel(tc, h_prev, x, w_last, b_last, w_out, b_out, out):
             hw[g] = hw_t
             hs[g] = hs_t
 
-        def pe_mm1(d):
+        def pe_mm1(d, part):
             g = d // 2
-            for t in (2 * (d % 2), 2 * (d % 2) + 1):
+            for t in (2 * (d % 2) + part,):
                 acc = psum.tile([P, 512], F32, name="acc", tag="A")
                 nc.tensor.matmul_mx(
                     out=acc[:],
@@ -220,8 +220,8 @@ def tile_deepfm_pa_t_kernel(tc, h_prev, x, w_last, b_last, w_out, b_out, out):
                 )
             tnat[d] = t_t
 
-        def pe_tT(d):
-            for jj in range(2):
+        def pe_tT(d, part):
+            for jj in (part,):
                 tbank[(d, jj)] = f32_to_psum(tnat[d], jj)
 
         def v_combine(d):
@@ -248,8 +248,8 @@ def tile_deepfm_pa_t_kernel(tc, h_prev, x, w_last, b_last, w_out, b_out, out):
             zw[d] = zw_t
             zs[d] = zs_t
 
-        def pe_mm2(d):
-            for jj in range(2):
+        def pe_mm2(d, part):
+            for jj in (part,):
                 acc2 = psum.tile([P, 512], F32, name="acc2", tag="O")
                 nc.tensor.matmul_mx(
                     out=acc2[:],
@@ -287,6 +287,8 @@ def tile_deepfm_pa_t_kernel(tc, h_prev, x, w_last, b_last, w_out, b_out, out):
         for i in range(NH + LAG_V4):
             if i % 2 == 0 and i // 2 + LOOKAHEAD < NG:
                 load(i // 2 + LOOKAHEAD)
+            if i % 2 == 0 and live(i - 2):
+                v_quant_h((i - 2) // 2)
             if live(i - LAG_V4):
                 v_bias_out(i - LAG_V4, 0)
             if live(i - LAG_QZ):
@@ -294,12 +296,10 @@ def tile_deepfm_pa_t_kernel(tc, h_prev, x, w_last, b_last, w_out, b_out, out):
             if live(i - LAG_V4):
                 v_bias_out(i - LAG_V4, 1)
                 store(i - LAG_V4)
-            if i % 2 == 0 and live(i - 2):
-                v_quant_h((i - 2) // 2)
             if live(i - LAG_S1):
                 s_relu(i - LAG_S1)
             if live(i - LAG_T):
-                pe_tT(i - LAG_T)
+                pe_tT(i - LAG_T, 0)
             if i == 1:
                 tb = psum.tile([P, 512], F32, name="tb", tag="T")
                 nc.tensor.transpose(out=tb[:, 0:128], in_=bl_f[:], identity=ident[:])
@@ -315,6 +315,16 @@ def tile_deepfm_pa_t_kernel(tc, h_prev, x, w_last, b_last, w_out, b_out, out):
                 nc.vector.quantize_mx(out=w2w[:].bitcast(FP8X4), scales=w2s[:], in_=gw2[:])
             if live(i):
                 pe_hT(i)
+            if live(i - LAG_MM1):
+                pe_mm1(i - LAG_MM1, 0)
+            if live(i - LAG_MM2):
+                pe_mm2(i - LAG_MM2, 0)
+            if live(i - LAG_T):
+                pe_tT(i - LAG_T, 1)
+            if live(i - LAG_MM1):
+                pe_mm1(i - LAG_MM1, 1)
+            if live(i - LAG_MM2):
+                pe_mm2(i - LAG_MM2, 1)
             if live(i - LAG_ROW):
                 s_rowsum(i - LAG_ROW)
                 g_scale(i - LAG_ROW)
@@ -322,7 +332,3 @@ def tile_deepfm_pa_t_kernel(tc, h_prev, x, w_last, b_last, w_out, b_out, out):
                 s_hT_out(i)
             if live(i - LAG_T):
                 v_combine(i - LAG_T)
-            if live(i - LAG_MM1):
-                pe_mm1(i - LAG_MM1)
-            if live(i - LAG_MM2):
-                pe_mm2(i - LAG_MM2)

@@ -21,14 +21,15 @@ GROUP = 512
 NG = B // GROUP
 NH = 2 * NG
 LOOKAHEAD = 3
+VECTOR_ROWSUMS = 4
 
 LAG_ROW = 1
 LAG_MM1 = 2
 LAG_S1 = 3
-LAG_T = 5
-LAG_QZ = 6
-LAG_MM2 = 6
-LAG_V4 = 7
+LAG_T = 4
+LAG_QZ = 5
+LAG_MM2 = 5
+LAG_V4 = 6
 
 
 def tile_deepfm_pa_t_kernel(tc, h_prev, x, w_last, b_last, w_out, b_out, out):
@@ -57,9 +58,9 @@ def tile_deepfm_pa_t_kernel(tc, h_prev, x, w_last, b_last, w_out, b_out, out):
             out=w1_raw[:].rearrange("p (ob k) -> p ob k", ob=4),
             in_=w_last.rearrange("(ob p) k -> p ob k", p=P),
         )
-        load(0)
         bl_bf = const.tile([P, P], BF16, name="bl_bf")
         nc.vector.memset(bl_bf[:].bitcast(I32), 0)
+        load(0)
         nc.sync.dma_start(out=bl_bf[0:4, :], in_=b_last.rearrange("(t p) -> t p", p=P))
         w2_raw = const.tile([P, 4 * D], BF16, name="w2_raw")
         nc.sync.dma_start(
@@ -71,6 +72,8 @@ def tile_deepfm_pa_t_kernel(tc, h_prev, x, w_last, b_last, w_out, b_out, out):
 
         ident = const.tile([P, P], F32, name="ident")
         masks.make_identity(nc, ident[:])
+        ident_bf = const.tile([P, P], BF16, name="ident_bf")
+        masks.make_identity(nc, ident_bf[:])
         bo = const.tile([P, D], BF16, name="bo")
         nc.sync.dma_start(out=bo[:], in_=b_out.partition_broadcast(P))
 
@@ -87,8 +90,8 @@ def tile_deepfm_pa_t_kernel(tc, h_prev, x, w_last, b_last, w_out, b_out, out):
                     )
             return bank
 
-        def words_out(bank, grouped, half):
-            nc.scalar.copy(
+        def words_out(bank, grouped, half, copy):
+            copy(
                 out=grouped[:].bitcast(F32)[:, 512 * half : 512 * half + 512].rearrange(
                     "p (j b u) -> p j b u", j=2, u=2
                 ),
@@ -110,24 +113,14 @@ def tile_deepfm_pa_t_kernel(tc, h_prev, x, w_last, b_last, w_out, b_out, out):
         w1s = const.tile([P, D], U8, name="w1s", align_bytes=64)
         for half in range(2):
             wb = words_to_psum(w1_raw[:].bitcast(F32), half)
-            words_out(wb, gw1, half)
+            words_out(wb, gw1, half, nc.scalar.copy if half == 0 else nc.vector.tensor_copy)
         nc.vector.quantize_mx(out=w1w[:].bitcast(FP8X4), scales=w1s[:], in_=gw1[:])
 
-        bl_f = const.tile([P, P], F32, name="bl_f")
-        nc.vector.tensor_copy(out=bl_f[:], in_=bl_bf[:])
         bh = const.tile([P, 4], F32, name="bh")
 
         gw2 = const.tile([P, 4 * D], BF16, name="gw2", align_bytes=64)
         w2w = const.tile([P, D], U32, name="w2w", align_bytes=64)
         w2s = const.tile([P, D], U8, name="w2s", align_bytes=64)
-        w2f = {}
-        for half in range(2):
-            wf = work.tile([P, 2 * D], F32, name="wf", tag="t", bufs=6)
-            nc.gpsimd.tensor_scalar(
-                out=wf[:], in0=w2_raw[:, 1024 * half : 1024 * half + 1024],
-                scalar1=1.0, scalar2=0.0, op0=ALU.mult, op1=ALU.add,
-            )
-            w2f[half] = wf
 
         hbank = {}
         gh = {}
@@ -152,7 +145,7 @@ def tile_deepfm_pa_t_kernel(tc, h_prev, x, w_last, b_last, w_out, b_out, out):
             if d % 2 == 0:
                 gh_t = work.tile([P, 4 * D], BF16, name="gh_t", tag="gh", bufs=2, align_bytes=64)
                 gh[g] = gh_t
-            words_out(hbank[d], gh[g], d % 2)
+            words_out(hbank[d], gh[g], d % 2, nc.scalar.copy)
 
         def v_quant_h(g):
             hw_t = work.tile([P, D], U32, name="hw_t", tag="hw", bufs=2, align_bytes=64)
@@ -190,19 +183,32 @@ def tile_deepfm_pa_t_kernel(tc, h_prev, x, w_last, b_last, w_out, b_out, out):
                     scale=0.5,
                 )
 
-        def s_rowsum(d):
+        def rowsum(d):
             g = d // 2
-            s_t = work.tile([P, 2], F32, name="s_t", tag="s", bufs=4)
+            on_vector = d < VECTOR_ROWSUMS
+            s_t = work.tile([P, 2], F32, name="s_t", tag="sv" if on_vector else "s", bufs=4)
             for jj in range(2):
                 j = 2 * (d % 2) + jj
-                junk = work.tile([P, D], BF16, name="junk", tag="junk", bufs=2)
-                nc.scalar.activation(
-                    out=junk[:],
-                    in_=x_in[g][:, 512 * j : 512 * j + 512],
-                    func=ACT.Copy,
-                    scale=0.5,
-                    accum_out=s_t[:, jj : jj + 1],
-                )
+                if on_vector:
+                    junk_v = work.tile([P, D], BF16, name="junk_v", tag="junk_v", bufs=2)
+                    nc.vector.tensor_scalar(
+                        out=junk_v[:],
+                        in0=x_in[g][:, 512 * j : 512 * j + 512],
+                        scalar1=0.5,
+                        scalar2=None,
+                        op0=ALU.mult,
+                        op1=ALU.add,
+                        accum_out=s_t[:, jj : jj + 1],
+                    )
+                else:
+                    junk = work.tile([P, D], BF16, name="junk", tag="junk", bufs=2)
+                    nc.scalar.activation(
+                        out=junk[:],
+                        in_=x_in[g][:, 512 * j : 512 * j + 512],
+                        func=ACT.Copy,
+                        scale=0.5,
+                        accum_out=s_t[:, jj : jj + 1],
+                    )
             ssum[d] = s_t
 
         def g_scale(d):
@@ -300,18 +306,23 @@ def tile_deepfm_pa_t_kernel(tc, h_prev, x, w_last, b_last, w_out, b_out, out):
                 s_relu(i - LAG_S1)
             if live(i - LAG_T):
                 pe_tT(i - LAG_T, 0)
-            if i == 1:
-                tb = psum.tile([P, 512], F32, name="tb", tag="T")
-                nc.tensor.transpose(out=tb[:, 0:128], in_=bl_f[:], identity=ident[:])
+            if i == 2:
+                tb = psum.tile([P, 1024], BF16, name="tb", tag="T")
+                nc.tensor.transpose(out=tb[:, 0:128], in_=bl_bf[:], identity=ident_bf[:])
                 nc.vector.tensor_scalar(out=bh[:], in0=tb[:, 0:4], scalar1=0.5, scalar2=None, op0=ALU.mult)
-            if 1 <= i <= 4:
-                ob = i - 1
-                wbank = f32_to_psum(w2f[ob // 2], ob % 2)
+            if 2 <= i <= 3:
+                half = i - 2
+                wbank = psum.tile([P, 1024], BF16, name="wbank", tag="T")
+                for q in range(8):
+                    col = 1024 * half + 128 * q
+                    nc.tensor.transpose(
+                        out=wbank[:, 128 * q : 128 * q + 128], in_=w2_raw[:, col : col + 128], identity=ident_bf[:]
+                    )
                 nc.vector.tensor_copy(
-                    out=gw2[:, 512 * ob : 512 * ob + 512].rearrange("p (o t) -> p o t", t=4),
-                    in_=wbank[:].rearrange("p (t o) -> p o t", t=4),
+                    out=gw2[:, 1024 * half : 1024 * half + 1024].rearrange("p (ob o t) -> p ob o t", ob=2, t=4),
+                    in_=wbank[:].rearrange("p (ob t o) -> p ob o t", ob=2, t=4),
                 )
-            if i == 5:
+            if i == 4:
                 nc.vector.quantize_mx(out=w2w[:].bitcast(FP8X4), scales=w2s[:], in_=gw2[:])
             if live(i):
                 pe_hT(i)
@@ -325,10 +336,10 @@ def tile_deepfm_pa_t_kernel(tc, h_prev, x, w_last, b_last, w_out, b_out, out):
                 pe_mm1(i - LAG_MM1, 1)
             if live(i - LAG_MM2):
                 pe_mm2(i - LAG_MM2, 1)
-            if live(i - LAG_ROW):
-                s_rowsum(i - LAG_ROW)
-                g_scale(i - LAG_ROW)
             if live(i):
                 s_hT_out(i)
+            if live(i - LAG_ROW):
+                rowsum(i - LAG_ROW)
+                g_scale(i - LAG_ROW)
             if live(i - LAG_T):
                 v_combine(i - LAG_T)

@@ -20,16 +20,18 @@ FLOPS = 2 * 2 * B * D * D
 GROUP = 512
 NG = B // GROUP
 NH = 2 * NG
-LOOKAHEAD = 3
-VECTOR_ROWSUMS = 4
+H_AHEAD = 3
+X_AHEAD = 1
 
-LAG_ROW = 1
-LAG_MM1 = 2
-LAG_S1 = 3
-LAG_T = 4
-LAG_QZ = 5
-LAG_MM2 = 5
-LAG_V4 = 6
+LAG_S2 = 1
+LAG_QH = 2
+LAG_ROW = 4
+LAG_MM1 = 4
+LAG_S1 = 5
+LAG_T = 7
+LAG_QZ = 8
+LAG_MM2 = 9
+LAG_V4 = 10
 
 
 def tile_deepfm_pa_t_kernel(tc, h_prev, x, w_last, b_last, w_out, b_out, out):
@@ -44,13 +46,16 @@ def tile_deepfm_pa_t_kernel(tc, h_prev, x, w_last, b_last, w_out, b_out, out):
         h_in = {}
         x_in = {}
 
-        def load(g):
-            rows = slice(GROUP * g, GROUP * (g + 1))
+        def load_h(g):
             h_t = io.tile([P, 4 * D], BF16, name="h_t", tag="h_in", bufs=4)
-            nc.sync.dma_start(out=h_t[:], in_=h_prev[rows, :].rearrange("(p j) k -> p (j k)", j=4))
-            x_t = io.tile([P, 4 * D], BF16, name="x_t", tag="x_in", bufs=5)
-            nc.sync.dma_start(out=x_t[:], in_=x[rows, :].rearrange("(p j) k -> p (j k)", j=4))
+            nc.sync.dma_start(
+                out=h_t[:], in_=h_prev[GROUP * g : GROUP * (g + 1), :].rearrange("(p j) k -> p (j k)", j=4)
+            )
             h_in[g] = h_t
+
+        def load_x(g):
+            x_t = io.tile([P, 4 * D], BF16, name="x_t", tag="x_in", bufs=5)
+            nc.sync.dma_start(out=x_t[:], in_=x[GROUP * g : GROUP * (g + 1), :].rearrange("(p j) k -> p (j k)", j=4))
             x_in[g] = x_t
 
         w1_raw = const.tile([P, 4 * D], BF16, name="w1_raw")
@@ -60,15 +65,16 @@ def tile_deepfm_pa_t_kernel(tc, h_prev, x, w_last, b_last, w_out, b_out, out):
         )
         bl_bf = const.tile([P, P], BF16, name="bl_bf")
         nc.vector.memset(bl_bf[:].bitcast(I32), 0)
-        load(0)
+        load_h(0)
         nc.sync.dma_start(out=bl_bf[0:4, :], in_=b_last.rearrange("(t p) -> t p", p=P))
         w2_raw = const.tile([P, 4 * D], BF16, name="w2_raw")
         nc.sync.dma_start(
             out=w2_raw[:].rearrange("p (ob k) -> p ob k", ob=4),
             in_=w_out.rearrange("(ob p) k -> p ob k", p=P),
         )
-        load(1)
-        load(2)
+        load_h(1)
+        load_x(0)
+        load_h(2)
 
         ident = const.tile([P, P], F32, name="ident")
         masks.make_identity(nc, ident[:])
@@ -77,18 +83,15 @@ def tile_deepfm_pa_t_kernel(tc, h_prev, x, w_last, b_last, w_out, b_out, out):
         bo = const.tile([P, D], BF16, name="bo")
         nc.sync.dma_start(out=bo[:], in_=b_out.partition_broadcast(P))
 
-        def words_to_psum(src_words, half):
-            bank = psum.tile([P, 512], F32, name="hbank", tag="H")
-            for jj in range(2):
-                for u in range(2):
-                    col = (2 * half + jj) * 256 + 128 * u
-                    dst = (2 * jj + u) * 128
-                    nc.tensor.transpose(
-                        out=bank[:, dst : dst + 128],
-                        in_=src_words[:, col : col + 128],
-                        identity=ident[:],
-                    )
-            return bank
+        def words_to_psum(bank, src_words, half, jj):
+            for u in range(2):
+                col = (2 * half + jj) * 256 + 128 * u
+                dst = (2 * jj + u) * 128
+                nc.tensor.transpose(
+                    out=bank[:, dst : dst + 128],
+                    in_=src_words[:, col : col + 128],
+                    identity=ident[:],
+                )
 
         def words_out(bank, grouped, half, copy):
             copy(
@@ -112,7 +115,9 @@ def tile_deepfm_pa_t_kernel(tc, h_prev, x, w_last, b_last, w_out, b_out, out):
         w1w = const.tile([P, D], U32, name="w1w", align_bytes=64)
         w1s = const.tile([P, D], U8, name="w1s", align_bytes=64)
         for half in range(2):
-            wb = words_to_psum(w1_raw[:].bitcast(F32), half)
+            wb = psum.tile([P, 512], F32, name="wb", tag="H")
+            words_to_psum(wb, w1_raw[:].bitcast(F32), half, 0)
+            words_to_psum(wb, w1_raw[:].bitcast(F32), half, 1)
             words_out(wb, gw1, half, nc.scalar.copy if half == 0 else nc.vector.tensor_copy)
         nc.vector.quantize_mx(out=w1w[:].bitcast(FP8X4), scales=w1s[:], in_=gw1[:])
 
@@ -137,19 +142,22 @@ def tile_deepfm_pa_t_kernel(tc, h_prev, x, w_last, b_last, w_out, b_out, out):
         obank = {}
         osb = {}
 
-        def pe_hT(d):
-            hbank[d] = words_to_psum(h_in[d // 2][:].bitcast(F32), d % 2)
+        def pe_hT(d, part):
+            if part == 0:
+                hb = psum.tile([P, 512], F32, name="hb", tag="H")
+                hbank[d] = hb
+            words_to_psum(hbank[d], h_in[d // 2][:].bitcast(F32), d % 2, part)
 
         def s_hT_out(d):
             g = d // 2
             if d % 2 == 0:
-                gh_t = work.tile([P, 4 * D], BF16, name="gh_t", tag="gh", bufs=2, align_bytes=64)
+                gh_t = work.tile([P, 4 * D], BF16, name="gh_t", tag="gh", bufs=3, align_bytes=64)
                 gh[g] = gh_t
             words_out(hbank[d], gh[g], d % 2, nc.scalar.copy)
 
         def v_quant_h(g):
-            hw_t = work.tile([P, D], U32, name="hw_t", tag="hw", bufs=2, align_bytes=64)
-            hs_t = work.tile([P, D], U8, name="hs_t", tag="hs", bufs=2, align_bytes=64)
+            hw_t = work.tile([P, D], U32, name="hw_t", tag="hw", bufs=3, align_bytes=64)
+            hs_t = work.tile([P, D], U8, name="hs_t", tag="hs", bufs=3, align_bytes=64)
             nc.vector.quantize_mx(out=hw_t[:].bitcast(FP8X4), scales=hs_t[:], in_=gh[g][:])
             hw[g] = hw_t
             hs[g] = hs_t
@@ -185,30 +193,17 @@ def tile_deepfm_pa_t_kernel(tc, h_prev, x, w_last, b_last, w_out, b_out, out):
 
         def rowsum(d):
             g = d // 2
-            on_vector = d < VECTOR_ROWSUMS
-            s_t = work.tile([P, 2], F32, name="s_t", tag="sv" if on_vector else "s", bufs=4)
+            s_t = work.tile([P, 2], F32, name="s_t", tag="s", bufs=4)
             for jj in range(2):
                 j = 2 * (d % 2) + jj
-                if on_vector:
-                    junk_v = work.tile([P, D], BF16, name="junk_v", tag="junk_v", bufs=2)
-                    nc.vector.tensor_scalar(
-                        out=junk_v[:],
-                        in0=x_in[g][:, 512 * j : 512 * j + 512],
-                        scalar1=0.5,
-                        scalar2=None,
-                        op0=ALU.mult,
-                        op1=ALU.add,
-                        accum_out=s_t[:, jj : jj + 1],
-                    )
-                else:
-                    junk = work.tile([P, D], BF16, name="junk", tag="junk", bufs=2)
-                    nc.scalar.activation(
-                        out=junk[:],
-                        in_=x_in[g][:, 512 * j : 512 * j + 512],
-                        func=ACT.Copy,
-                        scale=0.5,
-                        accum_out=s_t[:, jj : jj + 1],
-                    )
+                junk = work.tile([P, D], BF16, name="junk", tag="junk", bufs=2)
+                nc.scalar.activation(
+                    out=junk[:],
+                    in_=x_in[g][:, 512 * j : 512 * j + 512],
+                    func=ACT.Copy,
+                    scale=0.5,
+                    accum_out=s_t[:, jj : jj + 1],
+                )
             ssum[d] = s_t
 
         def g_scale(d):
@@ -291,55 +286,52 @@ def tile_deepfm_pa_t_kernel(tc, h_prev, x, w_last, b_last, w_out, b_out, out):
             return 0 <= d < NH
 
         for i in range(NH + LAG_V4):
-            if i % 2 == 0 and i // 2 + LOOKAHEAD < NG:
-                load(i // 2 + LOOKAHEAD)
-            if i % 2 == 0 and live(i - 2):
-                v_quant_h((i - 2) // 2)
+            if i % 2 == 0:
+                if i // 2 + H_AHEAD < NG:
+                    load_h(i // 2 + H_AHEAD)
+                if i // 2 + X_AHEAD < NG:
+                    load_x(i // 2 + X_AHEAD)
             if live(i - LAG_V4):
                 v_bias_out(i - LAG_V4, 0)
-            if live(i - LAG_QZ):
-                v_quant_z(i - LAG_QZ)
-            if live(i - LAG_V4):
                 v_bias_out(i - LAG_V4, 1)
                 store(i - LAG_V4)
+            if live(i - LAG_QZ):
+                v_quant_z(i - LAG_QZ)
+            if live(i - LAG_QH) and (i - LAG_QH) % 2 == 1:
+                v_quant_h((i - LAG_QH) // 2)
             if live(i - LAG_S1):
                 s_relu(i - LAG_S1)
-            if live(i - LAG_T):
-                pe_tT(i - LAG_T, 0)
-            if i == 2:
-                tb = psum.tile([P, 1024], BF16, name="tb", tag="T")
-                nc.tensor.transpose(out=tb[:, 0:128], in_=bl_bf[:], identity=ident_bf[:])
-                nc.vector.tensor_scalar(out=bh[:], in0=tb[:, 0:4], scalar1=0.5, scalar2=None, op0=ALU.mult)
-            if 2 <= i <= 3:
-                half = i - 2
-                wbank = psum.tile([P, 1024], BF16, name="wbank", tag="T")
-                for q in range(8):
-                    col = 1024 * half + 128 * q
-                    nc.tensor.transpose(
-                        out=wbank[:, 128 * q : 128 * q + 128], in_=w2_raw[:, col : col + 128], identity=ident_bf[:]
-                    )
-                nc.vector.tensor_copy(
-                    out=gw2[:, 1024 * half : 1024 * half + 1024].rearrange("p (ob o t) -> p ob o t", ob=2, t=4),
-                    in_=wbank[:].rearrange("p (ob t o) -> p ob o t", ob=2, t=4),
-                )
-            if i == 4:
-                nc.vector.quantize_mx(out=w2w[:].bitcast(FP8X4), scales=w2s[:], in_=gw2[:])
-            if live(i):
-                pe_hT(i)
-            if live(i - LAG_MM1):
-                pe_mm1(i - LAG_MM1, 0)
-            if live(i - LAG_MM2):
-                pe_mm2(i - LAG_MM2, 0)
-            if live(i - LAG_T):
-                pe_tT(i - LAG_T, 1)
-            if live(i - LAG_MM1):
-                pe_mm1(i - LAG_MM1, 1)
-            if live(i - LAG_MM2):
-                pe_mm2(i - LAG_MM2, 1)
-            if live(i):
-                s_hT_out(i)
+            if live(i - LAG_S2):
+                s_hT_out(i - LAG_S2)
             if live(i - LAG_ROW):
                 rowsum(i - LAG_ROW)
                 g_scale(i - LAG_ROW)
+            for part in range(2):
+                if live(i - LAG_T):
+                    pe_tT(i - LAG_T, part)
+                if part == 0 and i == 2:
+                    tb = psum.tile([P, 1024], BF16, name="tb", tag="T")
+                    nc.tensor.transpose(out=tb[:, 0:128], in_=bl_bf[:], identity=ident_bf[:])
+                    nc.vector.tensor_scalar(out=bh[:], in0=tb[:, 0:4], scalar1=0.5, scalar2=None, op0=ALU.mult)
+                if part == 0 and 3 <= i <= 4:
+                    half = i - 3
+                    wbank = psum.tile([P, 1024], BF16, name="wbank", tag="T")
+                    for q in range(8):
+                        col = 1024 * half + 128 * q
+                        nc.tensor.transpose(
+                            out=wbank[:, 128 * q : 128 * q + 128], in_=w2_raw[:, col : col + 128], identity=ident_bf[:]
+                        )
+                    nc.vector.tensor_copy(
+                        out=gw2[:, 1024 * half : 1024 * half + 1024].rearrange("p (ob o t) -> p ob o t", ob=2, t=4),
+                        in_=wbank[:].rearrange("p (ob t o) -> p ob o t", ob=2, t=4),
+                    )
+                if part == 0 and i == 5:
+                    nc.vector.quantize_mx(out=w2w[:].bitcast(FP8X4), scales=w2s[:], in_=gw2[:])
+                if live(i):
+                    pe_hT(i, part)
+                if live(i - LAG_MM1):
+                    pe_mm1(i - LAG_MM1, part)
+                if live(i - LAG_MM2):
+                    pe_mm2(i - LAG_MM2, part)
             if live(i - LAG_T):
                 v_combine(i - LAG_T)

@@ -32,6 +32,7 @@ LAG_T = 7
 LAG_QZ = 8
 LAG_MM2 = 9
 LAG_V4 = 10
+LAG_STORE = 11
 
 
 def tile_deepfm_pa_t_kernel(tc, h_prev, x, w_last, b_last, w_out, b_out, out):
@@ -263,16 +264,19 @@ def tile_deepfm_pa_t_kernel(tc, h_prev, x, w_last, b_last, w_out, b_out, out):
                 )
                 obank[(d, jj)] = acc2
 
-        def v_bias_out(d, jj):
+        def by_scalar(d, jj):
+            return d % 2 == 1 and jj == 1
+
+        def bias_out(d, jj):
             if jj == 0:
-                o_t = io.tile([P, 2 * D], F32, name="o_t", tag="o", bufs=4)
+                o_t = io.tile([P, 2 * D], F32, name="o_t", tag="o", bufs=5)
                 osb[d] = o_t
-            nc.vector.tensor_tensor(
-                out=osb[d][:, 512 * jj : 512 * jj + 512],
-                in0=obank[(d, jj)][:],
-                in1=bo[:],
-                op=ALU.add,
-            )
+            part = osb[d][:, 512 * jj : 512 * jj + 512]
+            if by_scalar(d, jj):
+                nc.scalar.copy(out=part, in_=obank[(d, jj)][:])
+                nc.gpsimd.tensor_tensor(out=part, in0=part, in1=bo[:], op=ALU.add)
+            else:
+                nc.vector.tensor_tensor(out=part, in0=obank[(d, jj)][:], in1=bo[:], op=ALU.add)
 
         def store(d):
             g = d // 2
@@ -285,16 +289,17 @@ def tile_deepfm_pa_t_kernel(tc, h_prev, x, w_last, b_last, w_out, b_out, out):
         def live(d):
             return 0 <= d < NH
 
-        for i in range(NH + LAG_V4):
+        for i in range(NH + LAG_STORE):
             if i % 2 == 0:
                 if i // 2 + H_AHEAD < NG:
                     load_h(i // 2 + H_AHEAD)
                 if i // 2 + X_AHEAD < NG:
                     load_x(i // 2 + X_AHEAD)
+            if live(i - LAG_STORE):
+                store(i - LAG_STORE)
             if live(i - LAG_V4):
-                v_bias_out(i - LAG_V4, 0)
-                v_bias_out(i - LAG_V4, 1)
-                store(i - LAG_V4)
+                bias_out(i - LAG_V4, 0)
+                bias_out(i - LAG_V4, 1)
             if live(i - LAG_QZ):
                 v_quant_z(i - LAG_QZ)
             if live(i - LAG_QH) and (i - LAG_QH) % 2 == 1:

@@ -23,16 +23,18 @@ NH = 2 * NG
 H_AHEAD = 3
 X_AHEAD = 1
 
-LAG_S2 = 1
-LAG_QH = 2
-LAG_ROW = 4
-LAG_MM1 = 4
-LAG_S1 = 5
-LAG_T = 7
-LAG_QZ = 8
-LAG_MM2 = 9
-LAG_V4 = 10
-LAG_STORE = 11
+PRESUMMED = 3
+
+LAG_QH = 1
+LAG_PRESUM = 2
+LAG_ROW = 3
+LAG_MM1 = 3
+LAG_S1 = 4
+LAG_T = 6
+LAG_QZ = 7
+LAG_MM2 = 8
+LAG_V4 = 9
+LAG_STORE = 10
 
 
 def tile_deepfm_pa_t_kernel(tc, h_prev, x, w_last, b_last, w_out, b_out, out):
@@ -68,13 +70,13 @@ def tile_deepfm_pa_t_kernel(tc, h_prev, x, w_last, b_last, w_out, b_out, out):
         nc.vector.memset(bl_bf[:].bitcast(I32), 0)
         load_h(0)
         nc.sync.dma_start(out=bl_bf[0:4, :], in_=b_last.rearrange("(t p) -> t p", p=P))
+        load_x(0)
+        load_h(1)
         w2_raw = const.tile([P, 4 * D], BF16, name="w2_raw")
         nc.sync.dma_start(
             out=w2_raw[:].rearrange("p (ob k) -> p ob k", ob=4),
             in_=w_out.rearrange("(ob p) k -> p ob k", p=P),
         )
-        load_h(1)
-        load_x(0)
         load_h(2)
 
         ident = const.tile([P, P], F32, name="ident")
@@ -116,7 +118,7 @@ def tile_deepfm_pa_t_kernel(tc, h_prev, x, w_last, b_last, w_out, b_out, out):
         w1w = const.tile([P, D], U32, name="w1w", align_bytes=64)
         w1s = const.tile([P, D], U8, name="w1s", align_bytes=64)
         for half in range(2):
-            wb = psum.tile([P, 512], F32, name="wb", tag="H")
+            wb = psum.tile([P, 512], F32, name="wb", tag="H", bufs=1)
             words_to_psum(wb, w1_raw[:].bitcast(F32), half, 0)
             words_to_psum(wb, w1_raw[:].bitcast(F32), half, 1)
             words_out(wb, gw1, half, nc.scalar.copy if half == 0 else nc.vector.tensor_copy)
@@ -129,6 +131,7 @@ def tile_deepfm_pa_t_kernel(tc, h_prev, x, w_last, b_last, w_out, b_out, out):
         w2s = const.tile([P, D], U8, name="w2s", align_bytes=64)
 
         hbank = {}
+        ybank = {}
         gh = {}
         hw = {}
         hs = {}
@@ -143,11 +146,11 @@ def tile_deepfm_pa_t_kernel(tc, h_prev, x, w_last, b_last, w_out, b_out, out):
         obank = {}
         osb = {}
 
-        def pe_hT(d, part):
-            if part == 0:
-                hb = psum.tile([P, 512], F32, name="hb", tag="H")
-                hbank[d] = hb
-            words_to_psum(hbank[d], h_in[d // 2][:].bitcast(F32), d % 2, part)
+        def pe_hT(d):
+            hb = psum.tile([P, 512], F32, name="hb", tag="H", bufs=1)
+            hbank[d] = hb
+            for jj in range(2):
+                words_to_psum(hb, h_in[d // 2][:].bitcast(F32), d % 2, jj)
 
         def s_hT_out(d):
             g = d // 2
@@ -178,12 +181,12 @@ def tile_deepfm_pa_t_kernel(tc, h_prev, x, w_last, b_last, w_out, b_out, out):
                 )
                 abank[(g, t)] = acc
 
-        def s_relu(d):
+        def s_relu(d, part):
             g = d // 2
-            if d % 2 == 0:
+            if d % 2 == 0 and part == 0:
                 hp_t = work.tile([P, 4 * D], F32, name="hp_t", tag="hp", bufs=3)
                 hp[g] = hp_t
-            for t in (2 * (d % 2), 2 * (d % 2) + 1):
+            for t in (2 * (d % 2) + part,):
                 nc.scalar.activation(
                     out=hp[g][:, 512 * t : 512 * t + 512],
                     in_=abank[(g, t)][:],
@@ -192,19 +195,44 @@ def tile_deepfm_pa_t_kernel(tc, h_prev, x, w_last, b_last, w_out, b_out, out):
                     scale=0.5,
                 )
 
+        def pe_presum(d):
+            g = d // 2
+            y_t = psum.tile([P, 256], F32, name="y_t", tag="Y", bufs=1)
+            for jj in range(2):
+                j = 2 * (d % 2) + jj
+                if j < PRESUMMED:
+                    for t in range(4):
+                        nc.tensor.matmul(
+                            out=y_t[:, 128 * jj : 128 * jj + 128],
+                            lhsT=ident_bf[:],
+                            rhs=x_in[g][:, 512 * j + 128 * t : 512 * j + 128 * t + 128],
+                            start=(t == 0),
+                            stop=(t == 3),
+                        )
+            ybank[d] = y_t
+
         def rowsum(d):
             g = d // 2
             s_t = work.tile([P, 2], F32, name="s_t", tag="s", bufs=4)
             for jj in range(2):
                 j = 2 * (d % 2) + jj
                 junk = work.tile([P, D], BF16, name="junk", tag="junk", bufs=2)
-                nc.scalar.activation(
-                    out=junk[:],
-                    in_=x_in[g][:, 512 * j : 512 * j + 512],
-                    func=ACT.Copy,
-                    scale=0.5,
-                    accum_out=s_t[:, jj : jj + 1],
-                )
+                if j < PRESUMMED:
+                    nc.scalar.activation(
+                        out=junk[:, 0:128],
+                        in_=ybank[d][:, 128 * jj : 128 * jj + 128],
+                        func=ACT.Copy,
+                        scale=0.5,
+                        accum_out=s_t[:, jj : jj + 1],
+                    )
+                else:
+                    nc.scalar.activation(
+                        out=junk[:],
+                        in_=x_in[g][:, 512 * j : 512 * j + 512],
+                        func=ACT.Copy,
+                        scale=0.5,
+                        accum_out=s_t[:, jj : jj + 1],
+                    )
             ssum[d] = s_t
 
         def g_scale(d):
@@ -226,10 +254,13 @@ def tile_deepfm_pa_t_kernel(tc, h_prev, x, w_last, b_last, w_out, b_out, out):
             for jj in (part,):
                 tbank[(d, jj)] = f32_to_psum(tnat[d], jj)
 
-        def v_combine(d):
+        def v_combine(d, part):
             g = d // 2
-            zg_t = work.tile([P, 2 * D], BF16, name="zg_t", tag="zg", bufs=3, align_bytes=64)
-            for jj in range(2):
+            if part == 0:
+                zg_new = work.tile([P, 2 * D], BF16, name="zg_new", tag="zg", bufs=3, align_bytes=64)
+                zg[d] = zg_new
+            zg_t = zg[d]
+            for jj in (part,):
                 j = 2 * (d % 2) + jj
                 nc.vector.scalar_tensor_tensor(
                     out=zg_t[:, 512 * jj : 512 * jj + 512].rearrange("p (b t) -> p b t", t=4),
@@ -241,7 +272,6 @@ def tile_deepfm_pa_t_kernel(tc, h_prev, x, w_last, b_last, w_out, b_out, out):
                     op0=ALU.max,
                     op1=ALU.add,
                 )
-            zg[d] = zg_t
 
         def v_quant_z(d):
             zw_t = work.tile([P, 256], U32, name="zw_t", tag="zw", bufs=3, align_bytes=64)
@@ -299,44 +329,56 @@ def tile_deepfm_pa_t_kernel(tc, h_prev, x, w_last, b_last, w_out, b_out, out):
                 store(i - LAG_STORE)
             if live(i - LAG_V4):
                 bias_out(i - LAG_V4, 0)
+            if live(i - LAG_S1):
+                s_relu(i - LAG_S1, 0)
+            if live(i - LAG_T):
+                pe_tT(i - LAG_T, 0)
+            if i == 2:
+                tb = psum.tile([P, 1024], BF16, name="tb", tag="T")
+                nc.tensor.transpose(out=tb[:, 0:128], in_=bl_bf[:], identity=ident_bf[:])
+                nc.vector.tensor_scalar(out=bh[:], in0=tb[:, 0:4], scalar1=0.5, scalar2=None, op0=ALU.mult)
+            if 3 <= i <= 4:
+                half = i - 3
+                wbank = psum.tile([P, 1024], BF16, name="wbank", tag="T")
+                for q in range(8):
+                    col = 1024 * half + 128 * q
+                    nc.tensor.transpose(
+                        out=wbank[:, 128 * q : 128 * q + 128], in_=w2_raw[:, col : col + 128], identity=ident_bf[:]
+                    )
+                nc.vector.tensor_copy(
+                    out=gw2[:, 1024 * half : 1024 * half + 1024].rearrange("p (ob o t) -> p ob o t", ob=2, t=4),
+                    in_=wbank[:].rearrange("p (ob t o) -> p ob o t", ob=2, t=4),
+                )
+            if i == 5:
+                nc.vector.quantize_mx(out=w2w[:].bitcast(FP8X4), scales=w2s[:], in_=gw2[:])
+            if live(i):
+                pe_hT(i)
+            if live(i - LAG_T):
+                v_combine(i - LAG_T, 0)
+            if live(i - LAG_ROW):
+                rowsum(i - LAG_ROW)
+                g_scale(i - LAG_ROW)
+            if live(i - LAG_MM1):
+                pe_mm1(i - LAG_MM1, 0)
+            if live(i - LAG_MM2):
+                pe_mm2(i - LAG_MM2, 0)
+            if live(i - LAG_S1):
+                s_relu(i - LAG_S1, 1)
+            if live(i - LAG_V4):
                 bias_out(i - LAG_V4, 1)
+            if live(i - LAG_T):
+                pe_tT(i - LAG_T, 1)
+            if live(i - LAG_PRESUM):
+                pe_presum(i - LAG_PRESUM)
             if live(i - LAG_QZ):
                 v_quant_z(i - LAG_QZ)
             if live(i - LAG_QH) and (i - LAG_QH) % 2 == 1:
                 v_quant_h((i - LAG_QH) // 2)
-            if live(i - LAG_S1):
-                s_relu(i - LAG_S1)
-            if live(i - LAG_S2):
-                s_hT_out(i - LAG_S2)
-            if live(i - LAG_ROW):
-                rowsum(i - LAG_ROW)
-                g_scale(i - LAG_ROW)
-            for part in range(2):
-                if live(i - LAG_T):
-                    pe_tT(i - LAG_T, part)
-                if part == 0 and i == 2:
-                    tb = psum.tile([P, 1024], BF16, name="tb", tag="T")
-                    nc.tensor.transpose(out=tb[:, 0:128], in_=bl_bf[:], identity=ident_bf[:])
-                    nc.vector.tensor_scalar(out=bh[:], in0=tb[:, 0:4], scalar1=0.5, scalar2=None, op0=ALU.mult)
-                if part == 0 and 3 <= i <= 4:
-                    half = i - 3
-                    wbank = psum.tile([P, 1024], BF16, name="wbank", tag="T")
-                    for q in range(8):
-                        col = 1024 * half + 128 * q
-                        nc.tensor.transpose(
-                            out=wbank[:, 128 * q : 128 * q + 128], in_=w2_raw[:, col : col + 128], identity=ident_bf[:]
-                        )
-                    nc.vector.tensor_copy(
-                        out=gw2[:, 1024 * half : 1024 * half + 1024].rearrange("p (ob o t) -> p ob o t", ob=2, t=4),
-                        in_=wbank[:].rearrange("p (ob t o) -> p ob o t", ob=2, t=4),
-                    )
-                if part == 0 and i == 5:
-                    nc.vector.quantize_mx(out=w2w[:].bitcast(FP8X4), scales=w2s[:], in_=gw2[:])
-                if live(i):
-                    pe_hT(i, part)
-                if live(i - LAG_MM1):
-                    pe_mm1(i - LAG_MM1, part)
-                if live(i - LAG_MM2):
-                    pe_mm2(i - LAG_MM2, part)
             if live(i - LAG_T):
-                v_combine(i - LAG_T)
+                v_combine(i - LAG_T, 1)
+            if live(i - LAG_MM1):
+                pe_mm1(i - LAG_MM1, 1)
+            if live(i - LAG_MM2):
+                pe_mm2(i - LAG_MM2, 1)
+            if live(i):
+                s_hT_out(i)

@@ -20,21 +20,25 @@ FLOPS = 2 * 2 * B * D * D
 GROUP = 512
 NG = B // GROUP
 NH = 2 * NG
+STEP = GROUP // 2
 H_AHEAD = 3
-X_AHEAD = 1
-
-PRESUMMED = 3
-
+X_AHEAD = 2
+HEAD = 0
+TAIL = 32
+BLOCK = 64
+SPLIT = 256
+DRAIN = 28
+W2_ROUND = 2
+LAG_PRE = 0
+LAG_ROW = 1
 LAG_QH = 1
-LAG_PRESUM = 2
-LAG_ROW = 3
-LAG_MM1 = 3
-LAG_S1 = 4
-LAG_T = 6
-LAG_QZ = 7
-LAG_MM2 = 8
-LAG_V4 = 9
-LAG_STORE = 10
+LAG_MM1 = 1
+LAG_RELU = 2
+LAG_T = 2
+LAG_QZ = 3
+LAG_MM2 = 3
+LAG_OUT = 4
+LAG_STORE = 5
 
 
 def tile_deepfm_pa_t_kernel(tc, h_prev, x, w_last, b_last, w_out, b_out, out):
@@ -49,83 +53,58 @@ def tile_deepfm_pa_t_kernel(tc, h_prev, x, w_last, b_last, w_out, b_out, out):
         h_in = {}
         x_in = {}
 
-        def load_h(g):
-            h_t = io.tile([P, 4 * D], BF16, name="h_t", tag="h_in", bufs=4)
-            nc.sync.dma_start(
-                out=h_t[:], in_=h_prev[GROUP * g : GROUP * (g + 1), :].rearrange("(p j) k -> p (j k)", j=4)
-            )
-            h_in[g] = h_t
-
-        def load_x(g):
-            x_t = io.tile([P, 4 * D], BF16, name="x_t", tag="x_in", bufs=5)
-            nc.sync.dma_start(out=x_t[:], in_=x[GROUP * g : GROUP * (g + 1), :].rearrange("(p j) k -> p (j k)", j=4))
-            x_in[g] = x_t
+        def load(src, store_in, g, name, halves):
+            if halves in (None, 0):
+                new = io.tile([P, 4 * D], BF16, name="new", tag=name, bufs=5)
+                store_in[g] = new
+            rows = src[GROUP * g : GROUP * (g + 1), :].rearrange("(p j) k -> p (j k)", j=4)
+            cols = slice(0, 4 * D) if halves is None else slice(2 * D * halves, 2 * D * (halves + 1))
+            nc.sync.dma_start(out=store_in[g][:, cols], in_=rows[:, cols])
 
         w1_raw = const.tile([P, 4 * D], BF16, name="w1_raw")
-        nc.sync.dma_start(
-            out=w1_raw[:].rearrange("p (ob k) -> p ob k", ob=4),
-            in_=w_last.rearrange("(ob p) k -> p ob k", p=P),
-        )
-        bl_bf = const.tile([P, P], BF16, name="bl_bf")
-        nc.vector.memset(bl_bf[:].bitcast(I32), 0)
-        load_h(0)
-        nc.sync.dma_start(out=bl_bf[0:4, :], in_=b_last.rearrange("(t p) -> t p", p=P))
-        load_x(0)
-        load_h(1)
         w2_raw = const.tile([P, 4 * D], BF16, name="w2_raw")
+        bl_bf = const.tile([P, P], BF16, name="bl_bf")
+        bo = const.tile([P, D], BF16, name="bo")
+        nc.vector.memset(bl_bf[:].bitcast(I32), 0)
+        load(h_prev, h_in, 0, "h_in", 0)
         nc.sync.dma_start(
-            out=w2_raw[:].rearrange("p (ob k) -> p ob k", ob=4),
-            in_=w_out.rearrange("(ob p) k -> p ob k", p=P),
+            out=w1_raw[:].rearrange("p (ob k) -> p ob k", ob=4), in_=w_last.rearrange("(ob p) k -> p ob k", p=P)
         )
-        load_h(2)
+        load(x, x_in, 0, "x_in", 0)
+        load(h_prev, h_in, 0, "h_in", 1)
+        nc.sync.dma_start(out=bl_bf[0:4, :], in_=b_last.rearrange("(t p) -> t p", p=P))
+        load(x, x_in, 0, "x_in", 1)
+        load(h_prev, h_in, 1, "h_in", None)
+        nc.sync.dma_start(
+            out=w2_raw[:].rearrange("p (ob k) -> p ob k", ob=4), in_=w_out.rearrange("(ob p) k -> p ob k", p=P)
+        )
+        load(x, x_in, 1, "x_in", None)
+        load(h_prev, h_in, 2, "h_in", None)
 
         ident = const.tile([P, P], F32, name="ident")
         masks.make_identity(nc, ident[:])
         ident_bf = const.tile([P, P], BF16, name="ident_bf")
         masks.make_identity(nc, ident_bf[:])
-        bo = const.tile([P, D], BF16, name="bo")
-        nc.sync.dma_start(out=bo[:], in_=b_out.partition_broadcast(P))
 
-        def words_to_psum(bank, src_words, half, jj):
-            for u in range(2):
-                col = (2 * half + jj) * 256 + 128 * u
-                dst = (2 * jj + u) * 128
-                nc.tensor.transpose(
-                    out=bank[:, dst : dst + 128],
-                    in_=src_words[:, col : col + 128],
-                    identity=ident[:],
-                )
+        def words_to_psum(bank, src_words, half):
+            for jj in range(2):
+                for u in range(2):
+                    col = (2 * half + jj) * 256 + 128 * u
+                    dst = (2 * jj + u) * 128
+                    nc.tensor.transpose(
+                        out=bank[:, dst : dst + 128], in_=src_words[:, col : col + 128], identity=ident[:]
+                    )
 
-        def words_out(bank, grouped, half, copy):
+        def words_out(bank, grouped, copy):
             copy(
-                out=grouped[:].bitcast(F32)[:, 512 * half : 512 * half + 512].rearrange(
-                    "p (j b u) -> p j b u", j=2, u=2
-                ),
+                out=grouped.bitcast(F32).rearrange("p (j b u) -> p j b u", j=2, u=2),
                 in_=bank[:].rearrange("p (j u b) -> p j b u", j=2, u=2),
             )
-
-        def f32_to_psum(src, jj):
-            bank = psum.tile([P, 512], F32, name="tbank", tag="T")
-            for t in range(4):
-                nc.tensor.transpose(
-                    out=bank[:, 128 * t : 128 * t + 128],
-                    in_=src[:, 512 * jj + 128 * t : 512 * jj + 128 * t + 128],
-                    identity=ident[:],
-                )
-            return bank
 
         gw1 = const.tile([P, 4 * D], BF16, name="gw1", align_bytes=64)
         w1w = const.tile([P, D], U32, name="w1w", align_bytes=64)
         w1s = const.tile([P, D], U8, name="w1s", align_bytes=64)
-        for half in range(2):
-            wb = psum.tile([P, 512], F32, name="wb", tag="H", bufs=1)
-            words_to_psum(wb, w1_raw[:].bitcast(F32), half, 0)
-            words_to_psum(wb, w1_raw[:].bitcast(F32), half, 1)
-            words_out(wb, gw1, half, nc.scalar.copy if half == 0 else nc.vector.tensor_copy)
-        nc.vector.quantize_mx(out=w1w[:].bitcast(FP8X4), scales=w1s[:], in_=gw1[:])
-
         bh = const.tile([P, 4], F32, name="bh")
-
         gw2 = const.tile([P, 4 * D], BF16, name="gw2", align_bytes=64)
         w2w = const.tile([P, D], U32, name="w2w", align_bytes=64)
         w2s = const.tile([P, D], U8, name="w2s", align_bytes=64)
@@ -146,127 +125,144 @@ def tile_deepfm_pa_t_kernel(tc, h_prev, x, w_last, b_last, w_out, b_out, out):
         obank = {}
         osb = {}
 
+        def x_cols(d, jj):
+            return x_in[d // 2][:, 1024 * (d % 2) + 512 * jj : 1024 * (d % 2) + 512 * jj + 512]
+
         def pe_hT(d):
             hb = psum.tile([P, 512], F32, name="hb", tag="H", bufs=1)
             hbank[d] = hb
-            for jj in range(2):
-                words_to_psum(hb, h_in[d // 2][:].bitcast(F32), d % 2, jj)
+            words_to_psum(hb, h_in[d // 2][:].bitcast(F32), d % 2)
 
-        def s_hT_out(d):
-            g = d // 2
-            if d % 2 == 0:
-                gh_t = work.tile([P, 4 * D], BF16, name="gh_t", tag="gh", bufs=3, align_bytes=64)
-                gh[g] = gh_t
-            words_out(hbank[d], gh[g], d % 2, nc.scalar.copy)
+        def hT_out(d):
+            gh_t = work.tile([P, 2 * D], BF16, name="gh_t", tag="gh", bufs=3, align_bytes=64)
+            gh[d] = gh_t
+            words_out(hbank[d], gh_t[:], nc.scalar.copy)
 
-        def v_quant_h(g):
-            hw_t = work.tile([P, D], U32, name="hw_t", tag="hw", bufs=3, align_bytes=64)
-            hs_t = work.tile([P, D], U8, name="hs_t", tag="hs", bufs=3, align_bytes=64)
-            nc.vector.quantize_mx(out=hw_t[:].bitcast(FP8X4), scales=hs_t[:], in_=gh[g][:])
-            hw[g] = hw_t
-            hs[g] = hs_t
+        def v_quant_h(d):
+            hw_t = work.tile([P, STEP], U32, name="hw_t", tag="hw", bufs=3, align_bytes=64)
+            hs_t = work.tile([P, STEP], U8, name="hs_t", tag="hs", bufs=3, align_bytes=64)
+            nc.vector.quantize_mx(out=hw_t[:].bitcast(FP8X4), scales=hs_t[:], in_=gh[d][:])
+            hw[d] = hw_t
+            hs[d] = hs_t
 
-        def pe_mm1(d, part):
-            g = d // 2
-            for t in (2 * (d % 2) + part,):
+        def pe_mm1(d):
+            for half in range(2):
                 acc = psum.tile([P, 512], F32, name="acc", tag="A")
-                nc.tensor.matmul_mx(
-                    out=acc[:],
-                    lhsT=w1w[:, 128 * t : 128 * t + 128].bitcast(FP8X4),
-                    lhsT_scale=w1s[:, 128 * t : 128 * t + 128],
-                    rhs=hw[g][:].bitcast(FP8X4),
-                    rhs_scale=hs[g][:],
-                    start=True,
-                    stop=True,
-                )
-                abank[(g, t)] = acc
+                for u in range(2):
+                    t = 2 * half + u
+                    nc.tensor.matmul_mx(
+                        out=acc[:, STEP * u : STEP * u + STEP],
+                        lhsT=w1w[:, 128 * t : 128 * t + 128].bitcast(FP8X4),
+                        lhsT_scale=w1s[:, 128 * t : 128 * t + 128],
+                        rhs=hw[d][:].bitcast(FP8X4),
+                        rhs_scale=hs[d][:],
+                        start=True,
+                        stop=True,
+                    )
+                abank[(d, half)] = acc
 
-        def s_relu(d, part):
-            g = d // 2
-            if d % 2 == 0 and part == 0:
-                hp_t = work.tile([P, 4 * D], F32, name="hp_t", tag="hp", bufs=3)
-                hp[g] = hp_t
-            for t in (2 * (d % 2) + part,):
+        def s_relu(d):
+            hp_t = work.tile([P, 4 * STEP], F32, name="hp_t", tag="hp", bufs=3)
+            hp[d] = hp_t
+            for t in range(4):
                 nc.scalar.activation(
-                    out=hp[g][:, 512 * t : 512 * t + 512],
-                    in_=abank[(g, t)][:],
+                    out=hp_t[:, STEP * t : STEP * t + STEP],
+                    in_=abank[(d, t // 2)][:, STEP * (t % 2) : STEP * (t % 2) + STEP],
                     func=ACT.Relu,
                     bias=bh[:, t : t + 1],
                     scale=0.5,
                 )
 
+        def by_tensor(d, jj):
+            return HEAD <= d < TAIL and not (d % 2 == 1 and jj == 1)
+
         def pe_presum(d):
-            g = d // 2
-            y_t = psum.tile([P, 256], F32, name="y_t", tag="Y", bufs=1)
+            y_t = psum.tile([P, 2 * BLOCK], F32, name="y_t", tag="Y", bufs=1)
+            blocks = D // BLOCK
             for jj in range(2):
-                j = 2 * (d % 2) + jj
-                if j < PRESUMMED:
-                    for t in range(4):
+                if by_tensor(d, jj):
+                    for t in range(blocks):
                         nc.tensor.matmul(
-                            out=y_t[:, 128 * jj : 128 * jj + 128],
+                            out=y_t[:, BLOCK * jj : BLOCK * jj + BLOCK],
                             lhsT=ident_bf[:],
-                            rhs=x_in[g][:, 512 * j + 128 * t : 512 * j + 128 * t + 128],
+                            rhs=x_cols(d, jj)[:, BLOCK * t : BLOCK * t + BLOCK],
                             start=(t == 0),
-                            stop=(t == 3),
+                            stop=(t == blocks - 1),
                         )
             ybank[d] = y_t
 
-        def rowsum(d):
-            g = d // 2
+        def v_rowsum(d):
+            full = work.tile([P, 2], F32, name="full", tag="full", bufs=2)
+            nc.vector.tensor_reduce(
+                out=full[:],
+                in_=x_in[d // 2][:, 1024 * (d % 2) : 1024 * (d % 2) + 1024].rearrange("p (j k) -> p j k", j=2),
+                axis=mybir.AxisListType.X,
+                op=ALU.add,
+            )
             s_t = work.tile([P, 2], F32, name="s_t", tag="s", bufs=4)
-            for jj in range(2):
-                j = 2 * (d % 2) + jj
-                junk = work.tile([P, D], BF16, name="junk", tag="junk", bufs=2)
-                if j < PRESUMMED:
-                    nc.scalar.activation(
-                        out=junk[:, 0:128],
-                        in_=ybank[d][:, 128 * jj : 128 * jj + 128],
-                        func=ACT.Copy,
-                        scale=0.5,
-                        accum_out=s_t[:, jj : jj + 1],
-                    )
-                else:
-                    nc.scalar.activation(
-                        out=junk[:],
-                        in_=x_in[g][:, 512 * j : 512 * j + 512],
-                        func=ACT.Copy,
-                        scale=0.5,
-                        accum_out=s_t[:, jj : jj + 1],
-                    )
+            nc.scalar.activation(out=s_t[:], in_=full[:], func=ACT.Copy, scale=0.5)
             ssum[d] = s_t
 
-        def g_scale(d):
-            g = d // 2
-            t_t = work.tile([P, 2 * D], F32, name="t_t", tag="t", bufs=6)
+        def rowsum(d):
+            s_t = work.tile([P, 2], F32, name="s_t", tag="s", bufs=4)
             for jj in range(2):
-                j = 2 * (d % 2) + jj
-                nc.gpsimd.tensor_scalar(
-                    out=t_t[:, 512 * jj : 512 * jj + 512],
-                    in0=x_in[g][:, 512 * j : 512 * j + 512],
-                    scalar1=ssum[d][:, jj : jj + 1],
-                    scalar2=0.0,
-                    op0=ALU.mult,
-                    op1=ALU.add,
+                junk = work.tile([P, D], BF16, name="junk", tag="junk", bufs=2)
+                if by_tensor(d, jj):
+                    width, source = BLOCK, ybank[d][:, BLOCK * jj : BLOCK * jj + BLOCK]
+                else:
+                    width, source = D, x_cols(d, jj)
+                nc.scalar.activation(
+                    out=junk[:, 0:width], in_=source, func=ACT.Copy, scale=0.5, accum_out=s_t[:, jj : jj + 1]
                 )
+            ssum[d] = s_t
+
+        def scaled_by_scalar(d, jj):
+            return d % 2 == 0 and jj == 0
+
+        def g_scale(d):
+            t_t = work.tile([P, 2 * D], F32, name="t_t", tag="t", bufs=4)
             tnat[d] = t_t
+            for jj in range(2):
+                if not scaled_by_scalar(d, jj):
+                    nc.gpsimd.tensor_scalar(
+                        out=t_t[:, 512 * jj : 512 * jj + 512],
+                        in0=x_cols(d, jj),
+                        scalar1=ssum[d][:, jj : jj + 1],
+                        scalar2=0.0,
+                        op0=ALU.mult,
+                        op1=ALU.add,
+                    )
 
-        def pe_tT(d, part):
-            for jj in (part,):
-                tbank[(d, jj)] = f32_to_psum(tnat[d], jj)
+        def s_scale(d):
+            for jj in range(2):
+                if scaled_by_scalar(d, jj):
+                    nc.scalar.activation(
+                        out=tnat[d][:, 512 * jj : 512 * jj + 512],
+                        in_=x_cols(d, jj),
+                        func=ACT.Copy,
+                        scale=ssum[d][:, jj : jj + 1],
+                    )
 
-        def v_combine(d, part):
-            g = d // 2
-            if part == 0:
-                zg_new = work.tile([P, 2 * D], BF16, name="zg_new", tag="zg", bufs=3, align_bytes=64)
-                zg[d] = zg_new
-            zg_t = zg[d]
-            for jj in (part,):
-                j = 2 * (d % 2) + jj
+        def pe_tT(d, jjs=(0, 1)):
+            for jj in jjs:
+                bank = psum.tile([P, 512], F32, name="tbank", tag="T")
+                for t in range(4):
+                    nc.tensor.transpose(
+                        out=bank[:, 128 * t : 128 * t + 128],
+                        in_=tnat[d][:, 512 * jj + 128 * t : 512 * jj + 128 * t + 128],
+                        identity=ident[:],
+                    )
+                tbank[(d, jj)] = bank
+
+        def v_combine(d):
+            zg_t = work.tile([P, 2 * D], BF16, name="zg_t", tag="zg", bufs=3, align_bytes=64)
+            zg[d] = zg_t
+            for jj in range(2):
                 nc.vector.scalar_tensor_tensor(
                     out=zg_t[:, 512 * jj : 512 * jj + 512].rearrange("p (b t) -> p b t", t=4),
                     in0=tbank[(d, jj)][:].rearrange("p (t b) -> p b t", t=4),
                     scalar=0.0,
-                    in1=hp[g][:].rearrange("p (t c) -> p t c", t=4)[:, :, 128 * j : 128 * j + 128].rearrange(
+                    in1=hp[d][:].rearrange("p (t c) -> p t c", t=4)[:, :, 128 * jj : 128 * jj + 128].rearrange(
                         "p t b -> p b t"
                     ),
                     op0=ALU.max,
@@ -274,14 +270,14 @@ def tile_deepfm_pa_t_kernel(tc, h_prev, x, w_last, b_last, w_out, b_out, out):
                 )
 
         def v_quant_z(d):
-            zw_t = work.tile([P, 256], U32, name="zw_t", tag="zw", bufs=3, align_bytes=64)
-            zs_t = work.tile([P, 256], U8, name="zs_t", tag="zs", bufs=3, align_bytes=64)
+            zw_t = work.tile([P, STEP], U32, name="zw_t", tag="zw", bufs=3, align_bytes=64)
+            zs_t = work.tile([P, STEP], U8, name="zs_t", tag="zs", bufs=3, align_bytes=64)
             nc.vector.quantize_mx(out=zw_t[:].bitcast(FP8X4), scales=zs_t[:], in_=zg[d][:])
             zw[d] = zw_t
             zs[d] = zs_t
 
-        def pe_mm2(d, part):
-            for jj in (part,):
+        def pe_mm2(d):
+            for jj in range(2):
                 acc2 = psum.tile([P, 512], F32, name="acc2", tag="O")
                 nc.tensor.matmul_mx(
                     out=acc2[:],
@@ -294,52 +290,73 @@ def tile_deepfm_pa_t_kernel(tc, h_prev, x, w_last, b_last, w_out, b_out, out):
                 )
                 obank[(d, jj)] = acc2
 
-        def by_scalar(d, jj):
-            return d % 2 == 1 and jj == 1
+        def split(d):
+            return SPLIT if d < DRAIN else 0
 
-        def bias_out(d, jj):
-            if jj == 0:
-                o_t = io.tile([P, 2 * D], F32, name="o_t", tag="o", bufs=5)
-                osb[d] = o_t
-            part = osb[d][:, 512 * jj : 512 * jj + 512]
-            if by_scalar(d, jj):
-                nc.scalar.copy(out=part, in_=obank[(d, jj)][:])
-                nc.gpsimd.tensor_tensor(out=part, in0=part, in1=bo[:], op=ALU.add)
-            else:
-                nc.vector.tensor_tensor(out=part, in0=obank[(d, jj)][:], in1=bo[:], op=ALU.add)
+        def copy_out(d):
+            o_t = io.tile([P, 2 * D], F32, name="o_t", tag="o", bufs=5)
+            osb[d] = o_t
+            c = split(d)
+            part = o_t[:, D + c : 2 * D]
+            nc.scalar.copy(out=part, in_=obank[(d, 1)][:, c:D])
+            nc.gpsimd.tensor_tensor(out=part, in0=part, in1=bo[:, c:D], op=ALU.add)
+
+        def bias_out(d):
+            o_t = osb[d]
+            nc.vector.tensor_tensor(out=o_t[:, 0:D], in0=obank[(d, 0)][:], in1=bo[:], op=ALU.add)
+            c = split(d)
+            if c:
+                nc.vector.tensor_tensor(out=o_t[:, D : D + c], in0=obank[(d, 1)][:, 0:c], in1=bo[:, 0:c], op=ALU.add)
 
         def store(d):
-            g = d // 2
+            rows = out[GROUP * (d // 2) : GROUP * (d // 2 + 1), :].rearrange("(p j) o -> p j o", j=4)
             r = d % 2
-            nc.sync.dma_start(
-                out=out[GROUP * g : GROUP * (g + 1), :].rearrange("(p j) o -> p j o", j=4)[:, 2 * r : 2 * r + 2, :],
-                in_=osb[d][:].rearrange("p (j o) -> p j o", j=2),
-            )
+            nc.sync.dma_start(out=rows[:, 2 * r : 2 * r + 2, :], in_=osb[d][:].rearrange("p (j o) -> p j o", j=2))
 
         def live(d):
             return 0 <= d < NH
 
+        pe_hT(0)
+        hT_out(0)
+        for half in range(2):
+            wb = psum.tile([P, 512], F32, name="wb", tag="A")
+            words_to_psum(wb, w1_raw[:].bitcast(F32), half)
+            words_out(wb, gw1[:, 1024 * half : 1024 * half + 1024], nc.scalar.copy if half == 0 else nc.vector.tensor_copy)
+        nc.vector.quantize_mx(out=w1w[:].bitcast(FP8X4), scales=w1s[:], in_=gw1[:])
+        nc.sync.dma_start(out=bo[:], in_=b_out.partition_broadcast(P))
+        tb = psum.tile([P, 1024], BF16, name="tb", tag="T")
+        nc.tensor.transpose(out=tb[:, 0:128], in_=bl_bf[:], identity=ident_bf[:])
+        nc.vector.tensor_scalar(out=bh[:], in0=tb[:, 0:4], scalar1=0.5, scalar2=None, op0=ALU.mult)
+
         for i in range(NH + LAG_STORE):
             if i % 2 == 0:
-                if i // 2 + H_AHEAD < NG:
-                    load_h(i // 2 + H_AHEAD)
-                if i // 2 + X_AHEAD < NG:
-                    load_x(i // 2 + X_AHEAD)
+                if 3 <= i // 2 + H_AHEAD < NG:
+                    load(h_prev, h_in, i // 2 + H_AHEAD, "h_in", None)
+                if 2 <= i // 2 + X_AHEAD < NG:
+                    load(x, x_in, i // 2 + X_AHEAD, "x_in", None)
             if live(i - LAG_STORE):
                 store(i - LAG_STORE)
-            if live(i - LAG_V4):
-                bias_out(i - LAG_V4, 0)
-            if live(i - LAG_S1):
-                s_relu(i - LAG_S1, 0)
+            if live(i - LAG_ROW) and i - LAG_ROW >= HEAD:
+                rowsum(i - LAG_ROW)
+            if live(i - LAG_ROW):
+                g_scale(i - LAG_ROW)
+            if live(i - LAG_QH):
+                v_quant_h(i - LAG_QH)
+            if live(i - LAG_QZ):
+                v_quant_z(i - LAG_QZ)
+            if live(i - LAG_RELU):
+                s_relu(i - LAG_RELU)
+            if live(i - LAG_OUT):
+                copy_out(i - LAG_OUT)
+            if live(i - LAG_OUT):
+                bias_out(i - LAG_OUT)
+            if 0 < i < NH:
+                pe_hT(i)
             if live(i - LAG_T):
-                pe_tT(i - LAG_T, 0)
-            if i == 2:
-                tb = psum.tile([P, 1024], BF16, name="tb", tag="T")
-                nc.tensor.transpose(out=tb[:, 0:128], in_=bl_bf[:], identity=ident_bf[:])
-                nc.vector.tensor_scalar(out=bh[:], in0=tb[:, 0:4], scalar1=0.5, scalar2=None, op0=ALU.mult)
-            if 3 <= i <= 4:
-                half = i - 3
-                wbank = psum.tile([P, 1024], BF16, name="wbank", tag="T")
+                pe_tT(i - LAG_T)
+            if W2_ROUND <= i < W2_ROUND + 2:
+                half = i - W2_ROUND
+                wbank = psum.tile([P, 1024], BF16, name="wbank", tag="O")
                 for q in range(8):
                     col = 1024 * half + 128 * q
                     nc.tensor.transpose(
@@ -349,36 +366,17 @@ def tile_deepfm_pa_t_kernel(tc, h_prev, x, w_last, b_last, w_out, b_out, out):
                     out=gw2[:, 1024 * half : 1024 * half + 1024].rearrange("p (ob o t) -> p ob o t", ob=2, t=4),
                     in_=wbank[:].rearrange("p (ob t o) -> p ob o t", ob=2, t=4),
                 )
-            if i == 5:
-                nc.vector.quantize_mx(out=w2w[:].bitcast(FP8X4), scales=w2s[:], in_=gw2[:])
-            if live(i):
-                pe_hT(i)
+                if half == 1:
+                    nc.vector.quantize_mx(out=w2w[:].bitcast(FP8X4), scales=w2s[:], in_=gw2[:])
             if live(i - LAG_T):
-                v_combine(i - LAG_T, 0)
+                v_combine(i - LAG_T)
             if live(i - LAG_ROW):
-                rowsum(i - LAG_ROW)
-                g_scale(i - LAG_ROW)
+                s_scale(i - LAG_ROW)
+            if 0 < i < NH:
+                hT_out(i)
+            if HEAD <= i - LAG_PRE < TAIL:
+                pe_presum(i - LAG_PRE)
             if live(i - LAG_MM1):
-                pe_mm1(i - LAG_MM1, 0)
+                pe_mm1(i - LAG_MM1)
             if live(i - LAG_MM2):
-                pe_mm2(i - LAG_MM2, 0)
-            if live(i - LAG_S1):
-                s_relu(i - LAG_S1, 1)
-            if live(i - LAG_V4):
-                bias_out(i - LAG_V4, 1)
-            if live(i - LAG_T):
-                pe_tT(i - LAG_T, 1)
-            if live(i - LAG_PRESUM):
-                pe_presum(i - LAG_PRESUM)
-            if live(i - LAG_QZ):
-                v_quant_z(i - LAG_QZ)
-            if live(i - LAG_QH) and (i - LAG_QH) % 2 == 1:
-                v_quant_h((i - LAG_QH) // 2)
-            if live(i - LAG_T):
-                v_combine(i - LAG_T, 1)
-            if live(i - LAG_MM1):
-                pe_mm1(i - LAG_MM1, 1)
-            if live(i - LAG_MM2):
-                pe_mm2(i - LAG_MM2, 1)
-            if live(i):
-                s_hT_out(i)
+                pe_mm2(i - LAG_MM2)

@@ -239,7 +239,7 @@ def tile_deepfm_pa_t_kernel(tc, h_prev, x, w_last, b_last, w_out, b_out, out):
                     nc.scalar.activation(
                         out=tnat[d][:, 512 * jj : 512 * jj + 512],
                         in_=x_cols(d, jj),
-                        func=ACT.Copy,
+                        func=ACT.Relu,
                         scale=ssum[d][:, jj : jj + 1],
                     )
 
@@ -258,16 +258,24 @@ def tile_deepfm_pa_t_kernel(tc, h_prev, x, w_last, b_last, w_out, b_out, out):
             zg_t = work.tile([P, 2 * D], BF16, name="zg_t", tag="zg", bufs=3, align_bytes=64)
             zg[d] = zg_t
             for jj in range(2):
-                nc.vector.scalar_tensor_tensor(
-                    out=zg_t[:, 512 * jj : 512 * jj + 512].rearrange("p (b t) -> p b t", t=4),
-                    in0=tbank[(d, jj)][:].rearrange("p (t b) -> p b t", t=4),
-                    scalar=0.0,
-                    in1=hp[d][:].rearrange("p (t c) -> p t c", t=4)[:, :, 128 * jj : 128 * jj + 128].rearrange(
-                        "p t b -> p b t"
-                    ),
-                    op0=ALU.max,
-                    op1=ALU.add,
-                )
+                out_part = zg_t[:, 512 * jj : 512 * jj + 512]
+                h_part = hp[d][:].rearrange("p (t r) -> p t r", t=4)[:, :, 128 * jj : 128 * jj + 128]
+                if scaled_by_scalar(d, jj):
+                    nc.vector.tensor_tensor(
+                        out=out_part.rearrange("p (c i t) -> p c t i", i=4, t=4),
+                        in0=tbank[(d, jj)][:].rearrange("p (t c i) -> p c t i", t=4, i=4),
+                        in1=h_part.rearrange("p t (c i) -> p c t i", i=4),
+                        op=ALU.add,
+                    )
+                else:
+                    nc.vector.scalar_tensor_tensor(
+                        out=out_part.rearrange("p (b t) -> p b t", t=4),
+                        in0=tbank[(d, jj)][:].rearrange("p (t b) -> p b t", t=4),
+                        scalar=0.0,
+                        in1=h_part.rearrange("p t b -> p b t"),
+                        op0=ALU.max,
+                        op1=ALU.add,
+                    )
 
         def v_quant_z(d):
             zw_t = work.tile([P, STEP], U32, name="zw_t", tag="zw", bufs=3, align_bytes=64)

@@ -22,11 +22,11 @@ NG = B // GROUP
 NH = 2 * NG
 STEP = GROUP // 2
 H_AHEAD = 3
-X_AHEAD = 2
+X_AHEAD = 3
 HEAD = 0
 TAIL = 32
 BLOCK = 64
-SPLIT = 256
+SPLIT = 128
 DRAIN = 28
 W2_ROUND = 2
 LAG_PRE = 0
@@ -66,6 +66,10 @@ def tile_deepfm_pa_t_kernel(tc, h_prev, x, w_last, b_last, w_out, b_out, out):
         bl_bf = const.tile([P, P], BF16, name="bl_bf")
         bo = const.tile([P, D], BF16, name="bo")
         nc.vector.memset(bl_bf[:].bitcast(I32), 0)
+        bo_row = const.tile([P, D], BF16, name="bo_row")
+        nc.gpsimd.memset(bo_row[:].bitcast(I32), 0)
+        ones = const.tile([P, P], BF16, name="ones")
+        nc.gpsimd.memset(ones[:], 1.0)
         load(h_prev, h_in, 0, "h_in", 0)
         nc.sync.dma_start(
             out=w1_raw[:].rearrange("p (ob k) -> p ob k", ob=4), in_=w_last.rearrange("(ob p) k -> p ob k", p=P)
@@ -73,6 +77,7 @@ def tile_deepfm_pa_t_kernel(tc, h_prev, x, w_last, b_last, w_out, b_out, out):
         load(x, x_in, 0, "x_in", 0)
         load(h_prev, h_in, 0, "h_in", 1)
         nc.sync.dma_start(out=bl_bf[0:4, :], in_=b_last.rearrange("(t p) -> t p", p=P))
+        nc.sync.dma_start(out=bo_row[0:1, :], in_=b_out.rearrange("(u o) -> u o", u=1))
         load(x, x_in, 0, "x_in", 1)
         load(h_prev, h_in, 1, "h_in", None)
         nc.sync.dma_start(
@@ -80,6 +85,7 @@ def tile_deepfm_pa_t_kernel(tc, h_prev, x, w_last, b_last, w_out, b_out, out):
         )
         load(x, x_in, 1, "x_in", None)
         load(h_prev, h_in, 2, "h_in", None)
+        load(x, x_in, 2, "x_in", None)
 
         ident = const.tile([P, P], F32, name="ident")
         masks.make_identity(nc, ident[:])
@@ -331,7 +337,6 @@ def tile_deepfm_pa_t_kernel(tc, h_prev, x, w_last, b_last, w_out, b_out, out):
             words_to_psum(wb, w1_raw[:].bitcast(F32), half)
             words_out(wb, gw1[:, 1024 * half : 1024 * half + 1024], nc.scalar.copy if half == 0 else nc.vector.tensor_copy)
         nc.vector.quantize_mx(out=w1w[:].bitcast(FP8X4), scales=w1s[:], in_=gw1[:])
-        nc.sync.dma_start(out=bo[:], in_=b_out.partition_broadcast(P))
         tb = psum.tile([P, 1024], BF16, name="tb", tag="T")
         nc.tensor.transpose(out=tb[:, 0:128], in_=bl_bf[:], identity=ident_bf[:])
         nc.vector.tensor_scalar(out=bh[:], in0=tb[:, 0:4], scalar1=0.5, scalar2=None, op0=ALU.mult)
@@ -340,7 +345,7 @@ def tile_deepfm_pa_t_kernel(tc, h_prev, x, w_last, b_last, w_out, b_out, out):
             if i % 2 == 0:
                 if 3 <= i // 2 + H_AHEAD < NG:
                     load(h_prev, h_in, i // 2 + H_AHEAD, "h_in", None)
-                if 2 <= i // 2 + X_AHEAD < NG:
+                if 3 <= i // 2 + X_AHEAD < NG:
                     load(x, x_in, i // 2 + X_AHEAD, "x_in", None)
             if live(i - LAG_STORE):
                 store(i - LAG_STORE)
@@ -362,6 +367,10 @@ def tile_deepfm_pa_t_kernel(tc, h_prev, x, w_last, b_last, w_out, b_out, out):
                 pe_hT(i)
             if live(i - LAG_T):
                 pe_tT(i - LAG_T)
+            if i == 1:
+                bo_bank = psum.tile([P, D], F32, name="bo_bank", tag="O")
+                nc.tensor.matmul(out=bo_bank[:], lhsT=ones[:], rhs=bo_row[:], start=True, stop=True)
+                nc.vector.tensor_copy(out=bo[:], in_=bo_bank[:])
             if W2_ROUND <= i < W2_ROUND + 2:
                 half = i - W2_ROUND
                 wbank = psum.tile([P, 1024], BF16, name="wbank", tag="O")

@@ -28,7 +28,7 @@ TAIL = 32
 BLOCK = 64
 SPLIT = 128
 DRAIN = 28
-W2_ROUND = 2
+W2_ROUND = 1
 LAG_PRE = 0
 LAG_ROW = 1
 LAG_QH = 1
@@ -70,19 +70,22 @@ def tile_deepfm_pa_t_kernel(tc, h_prev, x, w_last, b_last, w_out, b_out, out):
         nc.gpsimd.memset(bo_row[:].bitcast(I32), 0)
         ones = const.tile([P, P], BF16, name="ones")
         nc.gpsimd.memset(ones[:], 1.0)
+        w1_blocks = w_last.rearrange("(ob p) k -> p ob k", p=P)
+        for half in range(2):
+            nc.sync.dma_start(
+                out=w1_raw[:, 2 * D * half : 2 * D * (half + 1)].rearrange("p (ob k) -> p ob k", ob=2),
+                in_=w1_blocks[:, 2 * half : 2 * half + 2, :],
+            )
         load(h_prev, h_in, 0, "h_in", 0)
-        nc.sync.dma_start(
-            out=w1_raw[:].rearrange("p (ob k) -> p ob k", ob=4), in_=w_last.rearrange("(ob p) k -> p ob k", p=P)
-        )
         load(x, x_in, 0, "x_in", 0)
         load(h_prev, h_in, 0, "h_in", 1)
         nc.sync.dma_start(out=bl_bf[0:4, :], in_=b_last.rearrange("(t p) -> t p", p=P))
         nc.sync.dma_start(out=bo_row[0:1, :], in_=b_out.rearrange("(u o) -> u o", u=1))
         load(x, x_in, 0, "x_in", 1)
-        load(h_prev, h_in, 1, "h_in", None)
         nc.sync.dma_start(
             out=w2_raw[:].rearrange("p (ob k) -> p ob k", ob=4), in_=w_out.rearrange("(ob p) k -> p ob k", p=P)
         )
+        load(h_prev, h_in, 1, "h_in", None)
         load(x, x_in, 1, "x_in", None)
         load(h_prev, h_in, 2, "h_in", None)
         load(x, x_in, 2, "x_in", None)
@@ -115,6 +118,7 @@ def tile_deepfm_pa_t_kernel(tc, h_prev, x, w_last, b_last, w_out, b_out, out):
         w2w = const.tile([P, D], U32, name="w2w", align_bytes=64)
         w2s = const.tile([P, D], U8, name="w2s", align_bytes=64)
 
+        w2_bank = {}
         hbank = {}
         ybank = {}
         gh = {}
@@ -305,6 +309,8 @@ def tile_deepfm_pa_t_kernel(tc, h_prev, x, w_last, b_last, w_out, b_out, out):
                 obank[(d, jj)] = acc2
 
         def split(d):
+            if d == NH - 1:
+                return 256
             return SPLIT if d < DRAIN else 0
 
         def copy_out(d):
@@ -325,17 +331,21 @@ def tile_deepfm_pa_t_kernel(tc, h_prev, x, w_last, b_last, w_out, b_out, out):
         def store(d):
             rows = out[GROUP * (d // 2) : GROUP * (d // 2 + 1), :].rearrange("(p j) o -> p j o", j=4)
             r = d % 2
-            nc.sync.dma_start(out=rows[:, 2 * r : 2 * r + 2, :], in_=osb[d][:].rearrange("p (j o) -> p j o", j=2))
+            if d < NH - 1:
+                nc.sync.dma_start(out=rows[:, 2 * r : 2 * r + 2, :], in_=osb[d][:].rearrange("p (j o) -> p j o", j=2))
+            else:
+                for jj in range(2):
+                    nc.sync.dma_start(out=rows[:, 2 * r + jj, :], in_=osb[d][:, D * jj : D * jj + D])
 
         def live(d):
             return 0 <= d < NH
 
-        pe_hT(0)
-        hT_out(0)
         for half in range(2):
             wb = psum.tile([P, 512], F32, name="wb", tag="A")
             words_to_psum(wb, w1_raw[:].bitcast(F32), half)
-            words_out(wb, gw1[:, 1024 * half : 1024 * half + 1024], nc.scalar.copy if half == 0 else nc.vector.tensor_copy)
+            words_out(wb, gw1[:, 1024 * half : 1024 * half + 1024], nc.vector.tensor_copy if half == 0 else nc.scalar.copy)
+        pe_hT(0)
+        hT_out(0)
         nc.vector.quantize_mx(out=w1w[:].bitcast(FP8X4), scales=w1s[:], in_=gw1[:])
         tb = psum.tile([P, 1024], BF16, name="tb", tag="T")
         nc.tensor.transpose(out=tb[:, 0:128], in_=bl_bf[:], identity=ident_bf[:])
@@ -371,20 +381,13 @@ def tile_deepfm_pa_t_kernel(tc, h_prev, x, w_last, b_last, w_out, b_out, out):
                 bo_bank = psum.tile([P, D], F32, name="bo_bank", tag="O")
                 nc.tensor.matmul(out=bo_bank[:], lhsT=ones[:], rhs=bo_row[:], start=True, stop=True)
                 nc.vector.tensor_copy(out=bo[:], in_=bo_bank[:])
-            if W2_ROUND <= i < W2_ROUND + 2:
-                half = i - W2_ROUND
-                wbank = psum.tile([P, 1024], BF16, name="wbank", tag="O")
-                for q in range(8):
-                    col = 1024 * half + 128 * q
-                    nc.tensor.transpose(
-                        out=wbank[:, 128 * q : 128 * q + 128], in_=w2_raw[:, col : col + 128], identity=ident_bf[:]
+            if i == W2_ROUND + 1:
+                for half in range(2):
+                    nc.vector.tensor_copy(
+                        out=gw2[:, 1024 * half : 1024 * half + 1024].rearrange("p (ob o t) -> p ob o t", ob=2, t=4),
+                        in_=w2_bank[half][:].rearrange("p (ob t o) -> p ob o t", ob=2, t=4),
                     )
-                nc.vector.tensor_copy(
-                    out=gw2[:, 1024 * half : 1024 * half + 1024].rearrange("p (ob o t) -> p ob o t", ob=2, t=4),
-                    in_=wbank[:].rearrange("p (ob t o) -> p ob o t", ob=2, t=4),
-                )
-                if half == 1:
-                    nc.vector.quantize_mx(out=w2w[:].bitcast(FP8X4), scales=w2s[:], in_=gw2[:])
+                nc.vector.quantize_mx(out=w2w[:].bitcast(FP8X4), scales=w2s[:], in_=gw2[:])
             if live(i - LAG_T):
                 v_combine(i - LAG_T)
             if live(i - LAG_ROW):
@@ -397,3 +400,12 @@ def tile_deepfm_pa_t_kernel(tc, h_prev, x, w_last, b_last, w_out, b_out, out):
                 pe_mm1(i - LAG_MM1)
             if live(i - LAG_MM2):
                 pe_mm2(i - LAG_MM2)
+            if i == W2_ROUND:
+                for half in range(2):
+                    wbank = psum.tile([P, 1024], BF16, name="wbank", tag="O")
+                    w2_bank[half] = wbank
+                    for q in range(8):
+                        col = 1024 * half + 128 * q
+                        nc.tensor.transpose(
+                            out=wbank[:, 128 * q : 128 * q + 128], in_=w2_raw[:, col : col + 128], identity=ident_bf[:]
+                        )

from contextlib import ExitStack

import concourse.masks as masks
import concourse.mybir as mybir

F32 = mybir.dt.float32
BF16 = mybir.dt.bfloat16
I32 = mybir.dt.int32
U32 = mybir.dt.uint32
U8 = mybir.dt.uint8
FP8X4 = mybir.dt.float8_e4m3fn_x4
ALU = mybir.AluOpType
ACT = mybir.ActivationFunctionType

P = 128
B = 8192
D = 512
FLOPS = 2 * 2 * B * D * D

GROUP = 512
NG = B // GROUP
NH = 2 * NG
STEP = GROUP // 2
H_AHEAD = 3
X_AHEAD = 3
HEAD = 0
TAIL = 32
BLOCK = 64
SPLIT = 128
DRAIN = 28
W2_ROUND = 1
LAG_PRE = 0
LAG_ROW = 1
LAG_QH = 1
LAG_MM1 = 1
LAG_RELU = 2
LAG_T = 2
LAG_QZ = 3
LAG_MM2 = 3
LAG_OUT = 4
LAG_STORE = 5


def tile_deepfm_pa_t_kernel(tc, h_prev, x, w_last, b_last, w_out, b_out, out):
    nc = tc.nc
    with ExitStack() as ctx:
        const = ctx.enter_context(tc.tile_pool(name="const", bufs=1))
        io = ctx.enter_context(tc.tile_pool(name="io", bufs=4))
        work = ctx.enter_context(tc.tile_pool(name="work", bufs=2))
        psum = ctx.enter_context(tc.psum_pool(name="psum", bufs=2))
        ctx.enter_context(tc.manual_schedule())

        h_in = {}
        x_in = {}

        def load(src, store_in, g, name, halves):
            if halves in (None, 0):
                new = io.tile([P, 4 * D], BF16, name="new", tag=name, bufs=5)
                store_in[g] = new
            rows = src[GROUP * g : GROUP * (g + 1), :].rearrange("(p j) k -> p (j k)", j=4)
            cols = slice(0, 4 * D) if halves is None else slice(2 * D * halves, 2 * D * (halves + 1))
            nc.sync.dma_start(out=store_in[g][:, cols], in_=rows[:, cols])

        w1_raw = const.tile([P, 4 * D], BF16, name="w1_raw")
        w2_raw = const.tile([P, 4 * D], BF16, name="w2_raw")
        bl_bf = const.tile([P, P], BF16, name="bl_bf")
        bo = const.tile([P, D], BF16, name="bo")
        nc.vector.memset(bl_bf[:].bitcast(I32), 0)
        bo_row = const.tile([P, D], BF16, name="bo_row")
        nc.gpsimd.memset(bo_row[:].bitcast(I32), 0)
        ones = const.tile([P, P], BF16, name="ones")
        nc.gpsimd.memset(ones[:], 1.0)
        w1_blocks = w_last.rearrange("(ob p) k -> p ob k", p=P)
        for half in range(2):
            nc.sync.dma_start(
                out=w1_raw[:, 2 * D * half : 2 * D * (half + 1)].rearrange("p (ob k) -> p ob k", ob=2),
                in_=w1_blocks[:, 2 * half : 2 * half + 2, :],
            )
        load(h_prev, h_in, 0, "h_in", 0)
        load(x, x_in, 0, "x_in", 0)
        load(h_prev, h_in, 0, "h_in", 1)
        nc.sync.dma_start(out=bl_bf[0:4, :], in_=b_last.rearrange("(t p) -> t p", p=P))
        nc.sync.dma_start(out=bo_row[0:1, :], in_=b_out.rearrange("(u o) -> u o", u=1))
        load(x, x_in, 0, "x_in", 1)
        nc.sync.dma_start(
            out=w2_raw[:].rearrange("p (ob k) -> p ob k", ob=4), in_=w_out.rearrange("(ob p) k -> p ob k", p=P)
        )
        load(h_prev, h_in, 1, "h_in", None)
        load(x, x_in, 1, "x_in", None)
        load(h_prev, h_in, 2, "h_in", None)
        load(x, x_in, 2, "x_in", None)

        ident = const.tile([P, P], F32, name="ident")
        masks.make_identity(nc, ident[:])
        ident_bf = const.tile([P, P], BF16, name="ident_bf")
        masks.make_identity(nc, ident_bf[:])

        def words_to_psum(bank, src_words, half):
            for jj in range(2):
                for u in range(2):
                    col = (2 * half + jj) * 256 + 128 * u
                    dst = (2 * jj + u) * 128
                    nc.tensor.transpose(
                        out=bank[:, dst : dst + 128], in_=src_words[:, col : col + 128], identity=ident[:]
                    )

        def words_out(bank, grouped, copy):
            copy(
                out=grouped.bitcast(F32).rearrange("p (j b u) -> p j b u", j=2, u=2),
                in_=bank[:].rearrange("p (j u b) -> p j b u", j=2, u=2),
            )

        gw1 = const.tile([P, 4 * D], BF16, name="gw1", align_bytes=64)
        w1w = const.tile([P, D], U32, name="w1w", align_bytes=64)
        w1s = const.tile([P, D], U8, name="w1s", align_bytes=64)
        bh = const.tile([P, 4], F32, name="bh")
        gw2 = const.tile([P, 4 * D], BF16, name="gw2", align_bytes=64)
        w2w = const.tile([P, D], U32, name="w2w", align_bytes=64)
        w2s = const.tile([P, D], U8, name="w2s", align_bytes=64)

        w2_bank = {}
        hbank = {}
        ybank = {}
        gh = {}
        hw = {}
        hs = {}
        abank = {}
        hp = {}
        ssum = {}
        tnat = {}
        tbank = {}
        zg = {}
        zw = {}
        zs = {}
        obank = {}
        osb = {}

        def x_cols(d, jj):
            return x_in[d // 2][:, 1024 * (d % 2) + 512 * jj : 1024 * (d % 2) + 512 * jj + 512]

        def pe_hT(d):
            hb = psum.tile([P, 512], F32, name="hb", tag="H", bufs=1)
            hbank[d] = hb
            words_to_psum(hb, h_in[d // 2][:].bitcast(F32), d % 2)

        def hT_out(d):
            gh_t = work.tile([P, 2 * D], BF16, name="gh_t", tag="gh", bufs=3, align_bytes=64)
            gh[d] = gh_t
            words_out(hbank[d], gh_t[:], nc.scalar.copy)

        def v_quant_h(d):
            hw_t = work.tile([P, STEP], U32, name="hw_t", tag="hw", bufs=3, align_bytes=64)
            hs_t = work.tile([P, STEP], U8, name="hs_t", tag="hs", bufs=3, align_bytes=64)
            nc.vector.quantize_mx(out=hw_t[:].bitcast(FP8X4), scales=hs_t[:], in_=gh[d][:])
            hw[d] = hw_t
            hs[d] = hs_t

        def pe_mm1(d):
            for half in range(2):
                acc = psum.tile([P, 512], F32, name="acc", tag="A")
                for u in range(2):
                    t = 2 * half + u
                    nc.tensor.matmul_mx(
                        out=acc[:, STEP * u : STEP * u + STEP],
                        lhsT=w1w[:, 128 * t : 128 * t + 128].bitcast(FP8X4),
                        lhsT_scale=w1s[:, 128 * t : 128 * t + 128],
                        rhs=hw[d][:].bitcast(FP8X4),
                        rhs_scale=hs[d][:],
                        start=True,
                        stop=True,
                    )
                abank[(d, half)] = acc

        def s_relu(d):
            hp_t = work.tile([P, 4 * STEP], F32, name="hp_t", tag="hp", bufs=3)
            hp[d] = hp_t
            for t in range(4):
                nc.scalar.activation(
                    out=hp_t[:, STEP * t : STEP * t + STEP],
                    in_=abank[(d, t // 2)][:, STEP * (t % 2) : STEP * (t % 2) + STEP],
                    func=ACT.Relu,
                    bias=bh[:, t : t + 1],
                    scale=0.5,
                )

        def by_tensor(d, jj):
            return HEAD <= d < TAIL and not (d % 2 == 1 and jj == 1)

        def pe_presum(d):
            y_t = psum.tile([P, 2 * BLOCK], F32, name="y_t", tag="Y", bufs=1)
            blocks = D // BLOCK
            for jj in range(2):
                if by_tensor(d, jj):
                    for t in range(blocks):
                        nc.tensor.matmul(
                            out=y_t[:, BLOCK * jj : BLOCK * jj + BLOCK],
                            lhsT=ident_bf[:],
                            rhs=x_cols(d, jj)[:, BLOCK * t : BLOCK * t + BLOCK],
                            start=(t == 0),
                            stop=(t == blocks - 1),
                        )
            ybank[d] = y_t

        def v_rowsum(d):
            full = work.tile([P, 2], F32, name="full", tag="full", bufs=2)
            nc.vector.tensor_reduce(
                out=full[:],
                in_=x_in[d // 2][:, 1024 * (d % 2) : 1024 * (d % 2) + 1024].rearrange("p (j k) -> p j k", j=2),
                axis=mybir.AxisListType.X,
                op=ALU.add,
            )
            s_t = work.tile([P, 2], F32, name="s_t", tag="s", bufs=4)
            nc.scalar.activation(out=s_t[:], in_=full[:], func=ACT.Copy, scale=0.5)
            ssum[d] = s_t

        def rowsum(d):
            s_t = work.tile([P, 2], F32, name="s_t", tag="s", bufs=4)
            for jj in range(2):
                junk = work.tile([P, D], BF16, name="junk", tag="junk", bufs=2)
                if by_tensor(d, jj):
                    width, source = BLOCK, ybank[d][:, BLOCK * jj : BLOCK * jj + BLOCK]
                else:
                    width, source = D, x_cols(d, jj)
                nc.scalar.activation(
                    out=junk[:, 0:width], in_=source, func=ACT.Copy, scale=0.5, accum_out=s_t[:, jj : jj + 1]
                )
            ssum[d] = s_t

        def scaled_by_scalar(d, jj):
            return d % 2 == 0 and jj == 0

        def g_scale(d):
            t_t = work.tile([P, 2 * D], F32, name="t_t", tag="t", bufs=4)
            tnat[d] = t_t
            for jj in range(2):
                if not scaled_by_scalar(d, jj):
                    nc.gpsimd.tensor_scalar(
                        out=t_t[:, 512 * jj : 512 * jj + 512],
                        in0=x_cols(d, jj),
                        scalar1=ssum[d][:, jj : jj + 1],
                        scalar2=0.0,
                        op0=ALU.mult,
                        op1=ALU.add,
                    )

        def s_scale(d):
            for jj in range(2):
                if scaled_by_scalar(d, jj):
                    nc.scalar.activation(
                        out=tnat[d][:, 512 * jj : 512 * jj + 512],
                        in_=x_cols(d, jj),
                        func=ACT.Relu,
                        scale=ssum[d][:, jj : jj + 1],
                    )

        def pe_tT(d, jjs=(0, 1)):
            for jj in jjs:
                bank = psum.tile([P, 512], F32, name="tbank", tag="T")
                for t in range(4):
                    nc.tensor.transpose(
                        out=bank[:, 128 * t : 128 * t + 128],
                        in_=tnat[d][:, 512 * jj + 128 * t : 512 * jj + 128 * t + 128],
                        identity=ident[:],
                    )
                tbank[(d, jj)] = bank

        def v_combine(d):
            zg_t = work.tile([P, 2 * D], BF16, name="zg_t", tag="zg", bufs=3, align_bytes=64)
            zg[d] = zg_t
            for jj in range(2):
                out_part = zg_t[:, 512 * jj : 512 * jj + 512]
                h_part = hp[d][:].rearrange("p (t r) -> p t r", t=4)[:, :, 128 * jj : 128 * jj + 128]
                if scaled_by_scalar(d, jj):
                    nc.vector.tensor_tensor(
                        out=out_part.rearrange("p (c i t) -> p c t i", i=4, t=4),
                        in0=tbank[(d, jj)][:].rearrange("p (t c i) -> p c t i", t=4, i=4),
                        in1=h_part.rearrange("p t (c i) -> p c t i", i=4),
                        op=ALU.add,
                    )
                else:
                    nc.vector.scalar_tensor_tensor(
                        out=out_part.rearrange("p (b t) -> p b t", t=4),
                        in0=tbank[(d, jj)][:].rearrange("p (t b) -> p b t", t=4),
                        scalar=0.0,
                        in1=h_part.rearrange("p t b -> p b t"),
                        op0=ALU.max,
                        op1=ALU.add,
                    )

        def v_quant_z(d):
            zw_t = work.tile([P, STEP], U32, name="zw_t", tag="zw", bufs=3, align_bytes=64)
            zs_t = work.tile([P, STEP], U8, name="zs_t", tag="zs", bufs=3, align_bytes=64)
            nc.vector.quantize_mx(out=zw_t[:].bitcast(FP8X4), scales=zs_t[:], in_=zg[d][:])
            zw[d] = zw_t
            zs[d] = zs_t

        def pe_mm2(d):
            for jj in range(2):
                acc2 = psum.tile([P, 512], F32, name="acc2", tag="O")
                nc.tensor.matmul_mx(
                    out=acc2[:],
                    lhsT=zw[d][:, 128 * jj : 128 * jj + 128].bitcast(FP8X4),
                    lhsT_scale=zs[d][:, 128 * jj : 128 * jj + 128],
                    rhs=w2w[:].bitcast(FP8X4),
                    rhs_scale=w2s[:],
                    start=True,
                    stop=True,
                )
                obank[(d, jj)] = acc2

        def split(d):
            if d == NH - 1:
                return 256
            return SPLIT if d < DRAIN else 0

        def copy_out(d):
            o_t = io.tile([P, 2 * D], F32, name="o_t", tag="o", bufs=5)
            osb[d] = o_t
            c = split(d)
            part = o_t[:, D + c : 2 * D]
            nc.scalar.copy(out=part, in_=obank[(d, 1)][:, c:D])
            nc.gpsimd.tensor_tensor(out=part, in0=part, in1=bo[:, c:D], op=ALU.add)

        def bias_out(d):
            o_t = osb[d]
            nc.vector.tensor_tensor(out=o_t[:, 0:D], in0=obank[(d, 0)][:], in1=bo[:], op=ALU.add)
            c = split(d)
            if c:
                nc.vector.tensor_tensor(out=o_t[:, D : D + c], in0=obank[(d, 1)][:, 0:c], in1=bo[:, 0:c], op=ALU.add)

        def store(d):
            rows = out[GROUP * (d // 2) : GROUP * (d // 2 + 1), :].rearrange("(p j) o -> p j o", j=4)
            r = d % 2
            if d < NH - 1:
                nc.sync.dma_start(out=rows[:, 2 * r : 2 * r + 2, :], in_=osb[d][:].rearrange("p (j o) -> p j o", j=2))
            else:
                for jj in range(2):
                    nc.sync.dma_start(out=rows[:, 2 * r + jj, :], in_=osb[d][:, D * jj : D * jj + D])

        def live(d):
            return 0 <= d < NH

        for half in range(2):
            wb = psum.tile([P, 512], F32, name="wb", tag="A")
            words_to_psum(wb, w1_raw[:].bitcast(F32), half)
            words_out(wb, gw1[:, 1024 * half : 1024 * half + 1024], nc.vector.tensor_copy if half == 0 else nc.scalar.copy)
        pe_hT(0)
        hT_out(0)
        nc.vector.quantize_mx(out=w1w[:].bitcast(FP8X4), scales=w1s[:], in_=gw1[:])
        tb = psum.tile([P, 1024], BF16, name="tb", tag="T")
        nc.tensor.transpose(out=tb[:, 0:128], in_=bl_bf[:], identity=ident_bf[:])
        nc.vector.tensor_scalar(out=bh[:], in0=tb[:, 0:4], scalar1=0.5, scalar2=None, op0=ALU.mult)

        for i in range(NH + LAG_STORE):
            if i % 2 == 0:
                if 3 <= i // 2 + H_AHEAD < NG:
                    load(h_prev, h_in, i // 2 + H_AHEAD, "h_in", None)
                if 3 <= i // 2 + X_AHEAD < NG:
                    load(x, x_in, i // 2 + X_AHEAD, "x_in", None)
            if live(i - LAG_STORE):
                store(i - LAG_STORE)
            if live(i - LAG_ROW) and i - LAG_ROW >= HEAD:
                rowsum(i - LAG_ROW)
            if live(i - LAG_ROW):
                g_scale(i - LAG_ROW)
            if live(i - LAG_QH):
                v_quant_h(i - LAG_QH)
            if live(i - LAG_QZ):
                v_quant_z(i - LAG_QZ)
            if live(i - LAG_RELU):
                s_relu(i - LAG_RELU)
            if live(i - LAG_OUT):
                copy_out(i - LAG_OUT)
            if live(i - LAG_OUT):
                bias_out(i - LAG_OUT)
            if 0 < i < NH:
                pe_hT(i)
            if live(i - LAG_T):
                pe_tT(i - LAG_T)
            if i == 1:
                bo_bank = psum.tile([P, D], F32, name="bo_bank", tag="O")
                nc.tensor.matmul(out=bo_bank[:], lhsT=ones[:], rhs=bo_row[:], start=True, stop=True)
                nc.vector.tensor_copy(out=bo[:], in_=bo_bank[:])
            if i == W2_ROUND + 1:
                for half in range(2):
                    nc.vector.tensor_copy(
                        out=gw2[:, 1024 * half : 1024 * half + 1024].rearrange("p (ob o t) -> p ob o t", ob=2, t=4),
                        in_=w2_bank[half][:].rearrange("p (ob t o) -> p ob o t", ob=2, t=4),
                    )
                nc.vector.quantize_mx(out=w2w[:].bitcast(FP8X4), scales=w2s[:], in_=gw2[:])
            if live(i - LAG_T):
                v_combine(i - LAG_T)
            if live(i - LAG_ROW):
                s_scale(i - LAG_ROW)
            if 0 < i < NH:
                hT_out(i)
            if HEAD <= i - LAG_PRE < TAIL:
                pe_presum(i - LAG_PRE)
            if live(i - LAG_MM1):
                pe_mm1(i - LAG_MM1)
            if live(i - LAG_MM2):
                pe_mm2(i - LAG_MM2)
            if i == W2_ROUND:
                for half in range(2):
                    wbank = psum.tile([P, 1024], BF16, name="wbank", tag="O")
                    w2_bank[half] = wbank
                    for q in range(8):
                        col = 1024 * half + 128 * q
                        nc.tensor.transpose(
                            out=wbank[:, 128 * q : 128 * q + 128], in_=w2_raw[:, col : col + 128], identity=ident_bf[:]
                        )
